import numpy as np
import ml_dtypes


def mxq(x, axis, fmt="e4m3"):
    dtype, down = {"e4m3": (ml_dtypes.float8_e4m3fn, 7), "e5m2": (ml_dtypes.float8_e5m2, 14)}[fmt]
    v = np.moveaxis(np.asarray(x, np.float32).astype(ml_dtypes.bfloat16).astype(np.float64), axis, -1)
    blocks = v.reshape(v.shape[:-1] + (-1, 32))
    amax = np.abs(blocks).max(-1, keepdims=True)
    byte = np.maximum(np.where(amax > 0, np.frexp(amax)[1] - 1 + 127, 0) - down, 1)
    scale = np.exp2(byte - 127.0)
    codes = (blocks / scale).astype(np.float32).astype(dtype).astype(np.float64)
    return np.moveaxis((codes * scale).reshape(v.shape), -1, axis)


WIDE = False


def mx_kscale(k):
    if not WIDE:
        return np.ones(k)
    levels = np.array([10, -10, 5, -5, 0])
    if k % 512:
        return np.exp2(np.random.permutation(np.resize(levels, k // 32))).repeat(32)
    a = np.empty((k // 512, 16))
    for p in range(k // 512):
        a[p, :8] = np.random.permutation(np.resize(levels, 8))
        for g in range(8):
            far = levels[np.abs(levels - a[p, g]) >= 10]
            a[p, g + 8] = far[np.random.randint(len(far))]
    return np.exp2(a.ravel()).repeat(32)


BF16 = ml_dtypes.bfloat16


def bf(x):
    return np.asarray(x, np.float32).astype(BF16)


def f64(x):
    return np.asarray(x).astype(np.float64)


B, S, D, E, F = 4, 1024, 512, 1024, 256
EPS = 1e-5


def layernorm(x, g, b):
    m = x.mean(-1, keepdims=True)
    v = ((x - m) ** 2).mean(-1, keepdims=True)
    return (x - m) * (1.0 / np.sqrt(v + EPS)) * g + b


def setup_inputs():
    s, t = mx_kscale(E), mx_kscale(D)
    return {"attn": bf(0.4 * np.random.standard_normal((B, S, E)) * s),
            "src_norm": bf(np.random.standard_normal((B, S, D)) + 0.3),
            "Wo": bf(np.random.standard_normal((D, E)) / np.sqrt(E) / s[None, :]),
            "bo": bf(0.1 * np.random.standard_normal(D)),
            "g2": bf((1.0 + 0.1 * np.random.standard_normal(D)) * t),
            "be2": bf(0.1 * np.random.standard_normal(D) * t),
            "W1": bf(np.random.standard_normal((F, D)) / np.sqrt(D) / t[None, :]),
            "b1": bf(0.1 * np.random.standard_normal(F))}


def reference(attn, src_norm, Wo, bo, g2, be2, W1, b1):
    x = f64(src_norm) + (mxq(f64(attn), 2, "e4m3") @ mxq(f64(Wo), 1, "e4m3").T) + f64(bo)
    h = layernorm(x, f64(g2), f64(be2))
    u = np.maximum((mxq(h, 2, "e4m3") @ mxq(f64(W1), 1, "e4m3").T) + f64(b1), 0.0)
    return x, u

@@ -1,0 +1,370 @@
+from contextlib import ExitStack
+
+import concourse.mybir as mybir
+from concourse.masks import make_identity
+
+F32 = mybir.dt.float32
+BF16 = mybir.dt.bfloat16
+U32 = mybir.dt.uint32
+U8 = mybir.dt.uint8
+FP8X4 = mybir.dt.float8_e4m3fn_x4
+ALU = mybir.AluOpType
+ACT = mybir.ActivationFunctionType
+
+P = 128
+PACK = 4
+K_PASS = P * PACK
+TOKENS, E, D, F = 4096, 1024, 512, 256
+EPS = 1e-5
+E_PASSES = E // K_PASS
+J = 2
+GROUP = J * P
+N_GROUPS = TOKENS // GROUP
+LOAD_AHEAD = 8
+TR_BANKS = 4
+SECOND_LAYER_ROUND = -3
+FLOPS = 2 * TOKENS * (E * D + D * F)
+
+
+def transpose_words(nc, bank, rows, ident):
+    for b in range(rows.shape[1] // P):
+        first = (b // 2) * 2 * P + b % 2
+        nc.tensor.transpose(bank[:, b, :], rows[:, first : first + 2 * P - 1 : 2], ident)
+
+
+def words_side_by_side(bank):
+    return bank.rearrange("p (g u) c -> p g c u", u=2)
+
+
+def tile_rotaryembeddingtransformerlayer_pb_t_kernel(
+    tc, attn, src_norm, Wo, bo, g2, be2, W1, b1, out_0, out_1
+):
+    nc = tc.nc
+    attn_groups = attn.flatten_outer_dims().rearrange("(n p j) k -> n p j k", p=P, j=J)
+    src_groups = src_norm.flatten_outer_dims().rearrange("(n p j) d -> n p j d", p=P, j=J)
+    x_groups = out_0.flatten_outer_dims().rearrange("(n p j) d -> n p j d", p=P, j=J)
+    u_groups = out_1.flatten_outer_dims().rearrange("(n p j) f -> n p j f", p=P, j=J)
+
+    with ExitStack() as ctx:
+        ctx.enter_context(tc.manual_schedule())
+        const = ctx.enter_context(tc.tile_pool(name="const", bufs=1))
+        loads = ctx.enter_context(tc.tile_pool(name="loads", bufs=5))
+        work = ctx.enter_context(tc.tile_pool(name="work", bufs=2))
+        x_pool = ctx.enter_context(tc.tile_pool(name="x_pool", bufs=5))
+        u_pool = ctx.enter_context(tc.tile_pool(name="u_pool", bufs=3))
+        stats = ctx.enter_context(tc.tile_pool(name="stats", bufs=4))
+        psum = ctx.enter_context(tc.psum_pool(name="psum", bufs=2))
+
+        ident = const.tile([P, P], F32)
+        make_identity(nc, ident[:])
+        eps_col = const.tile([P, 1], F32)
+        nc.vector.memset(eps_col[:], EPS)
+
+        bias_rows = const.tile([P, D + F], BF16)
+        nc.vector.memset(bias_rows[:], 0.0)
+        nc.scalar.dma_start(out=bias_rows[0:1, 0:D], in_=bo.rearrange("(o d) -> o d", o=1))
+        nc.scalar.dma_start(out=bias_rows[0:1, D : D + F], in_=b1.rearrange("(o f) -> o f", o=1))
+        ones = const.tile([P, P], BF16)
+        nc.vector.memset(ones[:], 1.0)
+        gain_bf16 = const.tile([P, PACK], BF16)
+        nc.scalar.dma_start(out=gain_bf16[:], in_=g2.rearrange("(p t) -> p t", t=PACK))
+        shift_bf16 = const.tile([P, PACK], BF16)
+        nc.scalar.dma_start(out=shift_bf16[:], in_=be2.rearrange("(p t) -> p t", t=PACK))
+        w1_rows = const.tile([P, F // P, D], BF16)
+        nc.scalar.dma_start(out=w1_rows[:], in_=W1.rearrange("(c p) d -> p c d", p=P))
+        table_warm = const.tile([P, 1], F32)
+        nc.scalar.activation(out=table_warm[:], in_=eps_col[:], func=ACT.Sqrt)
+        wo_rows = const.tile([P, D // P, E], BF16)
+        wo_chunks = Wo.rearrange("(c p) k -> c p k", p=P)
+        for c in range(D // P):
+            nc.sync.dma_start(out=wo_rows[:, c, :], in_=wo_chunks[c])
+
+        bo_bank = psum.tile([P, D], F32, tag="mm1")
+        nc.tensor.matmul(out=bo_bank[:], lhsT=ones[:], rhs=bias_rows[:, 0:D], start=True, stop=True)
+        bo_all = const.tile([P, D], F32)
+        nc.vector.tensor_copy(out=bo_all[:], in_=bo_bank[:])
+
+        wo_words = wo_rows[:].bitcast(F32)
+        wo_grouped = const.tile([P, E_PASSES, D, PACK], BF16, align_bytes=64)
+        wo_grouped_words = wo_grouped[:].bitcast(F32)
+        wo_codes = const.tile([P, E_PASSES, D], U32, align_bytes=64)
+        wo_scales = const.tile([P, E_PASSES, D], U8, align_bytes=64)
+
+        def quantise_wo_chunk(c):
+            rows_c = slice(c * P, (c + 1) * P)
+            for g in range(E_PASSES):
+                nc.vector.quantize_mx(
+                    out=wo_codes[:, g, rows_c].bitcast(FP8X4),
+                    scales=wo_scales[:, g, rows_c],
+                    in_=wo_grouped[:, g, rows_c, :].rearrange("p d t -> p (d t)"),
+                )
+
+        for c in range(D // P):
+            wo_bank = psum.tile([P, PACK, P], F32, tag="tr", bufs=TR_BANKS)
+            transpose_words(nc, wo_bank, wo_words[:, c, :], ident[:])
+            copy_out = nc.vector.tensor_copy if c % 2 == 0 else nc.scalar.copy
+            copy_out(out=wo_grouped_words[:, :, c * P : (c + 1) * P, :], in_=words_side_by_side(wo_bank[:]))
+            if c > 0:
+                quantise_wo_chunk(c - 1)
+        quantise_wo_chunk(D // P - 1)
+
+        b1_all = const.tile([P, F], F32)
+        gain_shift = const.tile([P, 2 * PACK], F32)
+        w1_codes = const.tile([P, F], U32, align_bytes=64)
+        w1_scales = const.tile([P, F], U8, align_bytes=64)
+
+        def prepare_second_layer():
+            b1_bank = psum.tile([P, F], F32, tag="mm2")
+            nc.tensor.matmul(out=b1_bank[:], lhsT=ones[:], rhs=bias_rows[:, D : D + F], start=True, stop=True)
+            nc.vector.tensor_copy(out=b1_all[:], in_=b1_bank[:])
+
+            nc.vector.tensor_copy(out=gain_shift[:, 0:PACK], in_=gain_bf16[:])
+            nc.vector.tensor_copy(out=gain_shift[:, PACK : 2 * PACK], in_=shift_bf16[:])
+
+            w1_words = w1_rows[:].bitcast(F32)
+            w1_grouped = const.tile([P, F, PACK], BF16, align_bytes=64)
+            w1_bank = psum.tile([P, F // P, 2, P], F32, tag="tr", bufs=TR_BANKS)
+            for c in range(F // P):
+                transpose_words(nc, w1_bank[:, c], w1_words[:, c, :], ident[:])
+            nc.vector.tensor_copy(
+                out=w1_grouped[:].bitcast(F32).rearrange("p (c f) u -> p c f u", c=F // P),
+                in_=w1_bank[:].rearrange("p c u f -> p c f u"),
+            )
+            nc.vector.quantize_mx(
+                out=w1_codes[:].bitcast(FP8X4),
+                scales=w1_scales[:],
+                in_=w1_grouped[:].rearrange("p f t -> p (f t)"),
+            )
+
+        attn_sb, src_sb, attn_banks, attn_grouped, attn_mx = {}, {}, {}, {}, {}
+        x_sb, x_banks, row_sum, sum_sq, std, inv_std, shift_z = {}, {}, {}, {}, {}, {}, {}
+        z_sb, z_banks, h_planes, h_grouped, h_mx, u_banks, u_sb = {}, {}, {}, {}, {}, {}, {}
+
+        def load(n):
+            attn_tile = loads.tile([P, J, E], BF16)
+            nc.sync.dma_start(out=attn_tile[:], in_=attn_groups[n])
+            src_tile = loads.tile([P, J, D], BF16)
+            nc.sync.dma_start(out=src_tile[:], in_=src_groups[n])
+            attn_sb[n], src_sb[n] = attn_tile, src_tile
+
+        def transpose_attn(n):
+            attn_words = attn_sb[n][:].bitcast(F32)
+            attn_banks[n] = []
+            for j in range(J):
+                attn_bank = psum.tile([P, PACK, P], F32, tag="tr", bufs=TR_BANKS)
+                transpose_words(nc, attn_bank, attn_words[:, j, :], ident[:])
+                attn_banks[n].append(attn_bank)
+
+        def copy_attn(n):
+            attn_side = work.tile([P, J, E_PASSES, P, PACK], BF16, align_bytes=64)
+            attn_side_words = attn_side[:].bitcast(F32)
+            for j in range(J):
+                nc.scalar.copy(out=attn_side_words[:, j, :, :, :], in_=words_side_by_side(attn_banks[n][j][:]))
+            attn_grouped[n] = attn_side
+
+        def quantise_attn(n):
+            attn_codes = work.tile([P, J, E_PASSES, P], U32, align_bytes=64)
+            attn_scales = work.tile([P, J, E_PASSES, P], U8, align_bytes=64)
+            nc.vector.quantize_mx(
+                out=attn_codes[:].rearrange("p j g k -> p (j g k)").bitcast(FP8X4),
+                scales=attn_scales[:].rearrange("p j g k -> p (j g k)"),
+                in_=attn_grouped[n][:].rearrange("p j g k t -> p (j g k t)"),
+            )
+            attn_mx[n] = (attn_codes, attn_scales)
+
+        def residual(n):
+            x_tile = x_pool.tile([P, J, D], F32)
+            nc.vector.tensor_tensor(
+                out=x_tile[:], in0=src_sb[n][:], in1=bo_all[:].unsqueeze(1).to_broadcast([P, J, D]), op=ALU.add
+            )
+            x_sb[n] = x_tile
+
+        def first_product(n):
+            codes, scales = attn_mx[n]
+            x_banks[n] = []
+            for j in range(J):
+                x_bank = psum.tile([P, D], F32, tag="mm1")
+                for g in range(E_PASSES):
+                    nc.tensor.matmul_mx(
+                        out=x_bank[:],
+                        lhsT=codes[:, j, g, :].bitcast(FP8X4),
+                        lhsT_scale=scales[:, j, g, :],
+                        rhs=wo_codes[:, g, :].bitcast(FP8X4),
+                        rhs_scale=wo_scales[:, g, :],
+                        start=(g == 0),
+                        stop=(g == E_PASSES - 1),
+                    )
+                x_banks[n].append(x_bank)
+
+        def finish_x(n, j):
+            if j == 0:
+                sum_tile = stats.tile([P, J], F32)
+                row_sum[n] = sum_tile
+            nc.vector.scalar_tensor_tensor(
+                out=x_sb[n][:, j, :],
+                in0=x_banks[n][j][:],
+                scalar=0.0,
+                in1=x_sb[n][:, j, :],
+                op0=ALU.add,
+                op1=ALU.add,
+                accum_out=row_sum[n][:, j : j + 1],
+            )
+
+        def store_x(n):
+            nc.sync.dma_start(out=x_groups[n], in_=x_sb[n][:])
+
+        def squared_deviations(n):
+            squares = work.tile([P, J, D], BF16)
+            sq_tile = stats.tile([P, J], F32)
+            for j in range(J):
+                nc.scalar.activation(
+                    out=squares[:, j, :],
+                    in_=x_sb[n][:, j, :],
+                    func=ACT.Square,
+                    scale=-float(D),
+                    bias=row_sum[n][:, j : j + 1],
+                    accum_out=sq_tile[:, j : j + 1],
+                )
+            sum_sq[n] = sq_tile
+
+        def standard_deviation(n):
+            std_tile = stats.tile([P, J], F32)
+            nc.scalar.activation(out=std_tile[:], in_=sum_sq[n][:], func=ACT.Sqrt, scale=1.0 / D**3, bias=eps_col[:])
+            std[n] = std_tile
+
+        def invert_std(n):
+            inv_tile = stats.tile([P, J], F32)
+            nc.vector.reciprocal(out=inv_tile[:], in_=std[n][:])
+            inv_std[n] = inv_tile
+
+        def shift_of_z(n):
+            shift_tile = stats.tile([P, J], F32)
+            nc.vector.scalar_tensor_tensor(
+                out=shift_tile[:], in0=row_sum[n][:], scalar=-1.0 / D, in1=inv_std[n][:], op0=ALU.mult, op1=ALU.mult
+            )
+            shift_z[n] = shift_tile
+
+        def normalise(n):
+            z_tile = work.tile([P, J, PACK, P], F32)
+            for j in range(J):
+                nc.scalar.activation(
+                    out=z_tile[:, j, :, :].rearrange("p t m -> p m t"),
+                    in_=x_sb[n][:, j, :].rearrange("p (m t) -> p m t", t=PACK),
+                    func=ACT.Identity,
+                    scale=inv_std[n][:, j : j + 1],
+                    bias=shift_z[n][:, j : j + 1],
+                )
+            z_sb[n] = z_tile
+
+        def transpose_z(n):
+            z_banks[n] = []
+            for half in range(PACK // 2):
+                z_bank = psum.tile([P, 2, GROUP], F32, tag="tr", bufs=TR_BANKS)
+                z_banks[n].append(z_bank)
+            for j in range(J):
+                for t in range(PACK):
+                    nc.tensor.transpose(
+                        z_banks[n][t // 2][:, t % 2, j * P : (j + 1) * P],
+                        z_sb[n][:, j, t, :],
+                        ident[:],
+                    )
+
+        def gain_and_shift(n):
+            planes = work.tile([P, PACK, GROUP], BF16)
+            for t in range(PACK):
+                nc.scalar.activation(
+                    out=planes[:, t, :],
+                    in_=z_banks[n][t // 2][:, t % 2, :],
+                    func=ACT.Identity,
+                    scale=gain_shift[:, t : t + 1],
+                    bias=gain_shift[:, PACK + t : PACK + t + 1],
+                )
+            h_planes[n] = planes
+
+        def regroup_h(n):
+            h_side = work.tile([P, GROUP, PACK], BF16, align_bytes=64)
+            nc.vector.tensor_copy(
+                out=h_side[:].rearrange("p (c i) t -> p c t i", i=4),
+                in_=h_planes[n][:].rearrange("p t (c i) -> p c t i", i=4),
+            )
+            h_grouped[n] = h_side
+
+        def quantise_h(n):
+            h_codes = work.tile([P, GROUP], U32, align_bytes=64)
+            h_scales = work.tile([P, GROUP], U8, align_bytes=64)
+            nc.vector.quantize_mx(
+                out=h_codes[:].bitcast(FP8X4), scales=h_scales[:], in_=h_grouped[n][:].rearrange("p k t -> p (k t)")
+            )
+            h_mx[n] = (h_codes, h_scales)
+
+        def second_product(n):
+            codes, scales = h_mx[n]
+            u_bank = psum.tile([P, J, F], F32, tag="mm2")
+            for j in range(J):
+                nc.tensor.matmul_mx(
+                    out=u_bank[:, j, :],
+                    lhsT=codes[:, j * P : (j + 1) * P].bitcast(FP8X4),
+                    lhsT_scale=scales[:, j * P : (j + 1) * P],
+                    rhs=w1_codes[:].bitcast(FP8X4),
+                    rhs_scale=w1_scales[:],
+                    start=True,
+                    stop=True,
+                )
+            u_banks[n] = u_bank
+
+        def add_b1(n):
+            u_tile = u_pool.tile([P, J, F], F32)
+            nc.vector.tensor_tensor(
+                out=u_tile[:], in0=u_banks[n][:], in1=b1_all[:].unsqueeze(1).to_broadcast([P, J, F]), op=ALU.add
+            )
+            u_sb[n] = u_tile
+
+        def relu_and_store_u(n):
+            nc.vector.tensor_scalar_max(out=u_sb[n][:], in0=u_sb[n][:], scalar1=0.0)
+            nc.sync.dma_start(out=u_groups[n], in_=u_sb[n][:])
+
+        def exists(n):
+            return 0 <= n < N_GROUPS
+
+        for r in range(-LOAD_AHEAD, N_GROUPS + 3):
+            if exists(r + 4):
+                transpose_attn(r + 4)
+            if exists(r + 1):
+                squared_deviations(r + 1)
+            if exists(r + 2):
+                finish_x(r + 2, 0)
+            if exists(r - 2):
+                quantise_h(r - 2)
+                second_product(r - 2)
+            if exists(r + 3):
+                quantise_attn(r + 3)
+            if exists(r - 3):
+                add_b1(r - 3)
+            if exists(r + 2):
+                finish_x(r + 2, 1)
+                store_x(r + 2)
+            if exists(r + 3):
+                first_product(r + 3)
+            if exists(r):
+                normalise(r)
+            if exists(r + 4):
+                residual(r + 4)
+            if exists(r + 1):
+                standard_deviation(r + 1)
+                invert_std(r + 1)
+            if exists(r - 1):
+                gain_and_shift(r - 1)
+            if exists(r):
+                transpose_z(r)
+            if exists(r - 3):
+                relu_and_store_u(r - 3)
+            if exists(r + 1):
+                shift_of_z(r + 1)
+            if exists(r - 1):
+                regroup_h(r - 1)
+            if exists(r + 4):
+                copy_attn(r + 4)
+            if exists(r + LOAD_AHEAD):
+                load(r + LOAD_AHEAD)
+            if r == SECOND_LAYER_ROUND:
+                prepare_second_layer()

@@ -73,7 +73,7 @@ def tile_rotaryembeddingtransformerlayer_pb_t_kernel(
         w1_rows = const.tile([P, F // P, D], BF16)
         nc.scalar.dma_start(out=w1_rows[:], in_=W1.rearrange("(c p) d -> p c d", p=P))
         table_warm = const.tile([P, 1], F32)
-        nc.scalar.activation(out=table_warm[:], in_=eps_col[:], func=ACT.Sqrt)
+        nc.scalar.activation(out=table_warm[:], in_=eps_col[:], func=ACT.Abs_reciprocal_sqrt)
         wo_rows = const.tile([P, D // P, E], BF16)
         wo_chunks = Wo.rearrange("(c p) k -> c p k", p=P)
         for c in range(D // P):
@@ -137,7 +137,7 @@ def tile_rotaryembeddingtransformerlayer_pb_t_kernel(
             )
 
         attn_sb, src_sb, attn_banks, attn_grouped, attn_mx = {}, {}, {}, {}, {}
-        x_sb, x_banks, row_sum, sum_sq, std, inv_std, shift_z = {}, {}, {}, {}, {}, {}, {}
+        x_sb, x_banks, row_sum, sum_sq, inv_std, mean = {}, {}, {}, {}, {}, {}
         z_sb, z_banks, h_planes, h_grouped, h_mx, u_banks, u_sb = {}, {}, {}, {}, {}, {}, {}
 
         def load(n):
@@ -227,32 +227,30 @@ def tile_rotaryembeddingtransformerlayer_pb_t_kernel(
                 )
             sum_sq[n] = sq_tile
 
-        def standard_deviation(n):
-            std_tile = stats.tile([P, J], F32)
-            nc.scalar.activation(out=std_tile[:], in_=sum_sq[n][:], func=ACT.Sqrt, scale=1.0 / D**3, bias=eps_col[:])
-            std[n] = std_tile
-
         def invert_std(n):
             inv_tile = stats.tile([P, J], F32)
-            nc.vector.reciprocal(out=inv_tile[:], in_=std[n][:])
+            nc.scalar.activation(
+                out=inv_tile[:], in_=sum_sq[n][:], func=ACT.Abs_reciprocal_sqrt, scale=1.0 / D**3, bias=eps_col[:]
+            )
             inv_std[n] = inv_tile
 
-        def shift_of_z(n):
-            shift_tile = stats.tile([P, J], F32)
-            nc.vector.scalar_tensor_tensor(
-                out=shift_tile[:], in0=row_sum[n][:], scalar=-1.0 / D, in1=inv_std[n][:], op0=ALU.mult, op1=ALU.mult
+        def mean_of_x(n):
+            mean_tile = stats.tile([P, J], F32)
+            nc.gpsimd.tensor_scalar(
+                out=mean_tile[:], in0=row_sum[n][:], scalar1=1.0 / D, scalar2=0.0, op0=ALU.mult, op1=ALU.add
             )
-            shift_z[n] = shift_tile
+            mean[n] = mean_tile
 
         def normalise(n):
             z_tile = work.tile([P, J, PACK, P], F32)
             for j in range(J):
-                nc.scalar.activation(
+                nc.gpsimd.tensor_scalar(
                     out=z_tile[:, j, :, :].rearrange("p t m -> p m t"),
-                    in_=x_sb[n][:, j, :].rearrange("p (m t) -> p m t", t=PACK),
-                    func=ACT.Identity,
-                    scale=inv_std[n][:, j : j + 1],
-                    bias=shift_z[n][:, j : j + 1],
+                    in0=x_sb[n][:, j, :].rearrange("p (m t) -> p m t", t=PACK),
+                    scalar1=mean[n][:, j : j + 1],
+                    scalar2=inv_std[n][:, j : j + 1],
+                    op0=ALU.subtract,
+                    op1=ALU.mult,
                 )
             z_sb[n] = z_tile
 
@@ -320,7 +318,7 @@ def tile_rotaryembeddingtransformerlayer_pb_t_kernel(
             u_sb[n] = u_tile
 
         def relu_and_store_u(n):
-            nc.vector.tensor_scalar_max(out=u_sb[n][:], in0=u_sb[n][:], scalar1=0.0)
+            nc.scalar.activation(out=u_sb[n][:], in_=u_sb[n][:], func=ACT.Relu)
             nc.sync.dma_start(out=u_groups[n], in_=u_sb[n][:])
 
         def exists(n):
@@ -350,7 +348,6 @@ def tile_rotaryembeddingtransformerlayer_pb_t_kernel(
             if exists(r + 4):
                 residual(r + 4)
             if exists(r + 1):
-                standard_deviation(r + 1)
                 invert_std(r + 1)
             if exists(r - 1):
                 gain_and_shift(r - 1)
@@ -359,7 +356,7 @@ def tile_rotaryembeddingtransformerlayer_pb_t_kernel(
             if exists(r - 3):
                 relu_and_store_u(r - 3)
             if exists(r + 1):
-                shift_of_z(r + 1)
+                mean_of_x(r + 1)
             if exists(r - 1):
                 regroup_h(r - 1)
             if exists(r + 4):

@@ -137,7 +137,7 @@ def tile_rotaryembeddingtransformerlayer_pb_t_kernel(
             )
 
         attn_sb, src_sb, attn_banks, attn_grouped, attn_mx = {}, {}, {}, {}, {}
-        x_sb, x_banks, row_sum, sum_sq, inv_std, mean = {}, {}, {}, {}, {}, {}
+        x_sb, x_banks, row_sum, sum_sq, inv_std, shift_z = {}, {}, {}, {}, {}, {}
         z_sb, z_banks, h_planes, h_grouped, h_mx, u_banks, u_sb = {}, {}, {}, {}, {}, {}, {}
 
         def load(n):
@@ -234,23 +234,25 @@ def tile_rotaryembeddingtransformerlayer_pb_t_kernel(
             )
             inv_std[n] = inv_tile
 
-        def mean_of_x(n):
+        def shift_of_z(n):
             mean_tile = stats.tile([P, J], F32)
             nc.gpsimd.tensor_scalar(
-                out=mean_tile[:], in0=row_sum[n][:], scalar1=1.0 / D, scalar2=0.0, op0=ALU.mult, op1=ALU.add
+                out=mean_tile[:], in0=row_sum[n][:], scalar1=-1.0 / D, scalar2=0.0, op0=ALU.mult, op1=ALU.add
             )
-            mean[n] = mean_tile
+            shift_tile = stats.tile([P, J], F32)
+            nc.gpsimd.tensor_tensor(out=shift_tile[:], in0=mean_tile[:], in1=inv_std[n][:], op=ALU.mult)
+            shift_z[n] = shift_tile
 
         def normalise(n):
-            z_tile = work.tile([P, J, PACK, P], F32)
+            z_tile = work.tile([P, J, D], F32)
             for j in range(J):
                 nc.gpsimd.tensor_scalar(
-                    out=z_tile[:, j, :, :].rearrange("p t m -> p m t"),
-                    in0=x_sb[n][:, j, :].rearrange("p (m t) -> p m t", t=PACK),
-                    scalar1=mean[n][:, j : j + 1],
-                    scalar2=inv_std[n][:, j : j + 1],
-                    op0=ALU.subtract,
-                    op1=ALU.mult,
+                    out=z_tile[:, j, :],
+                    in0=x_sb[n][:, j, :],
+                    scalar1=inv_std[n][:, j : j + 1],
+                    scalar2=shift_z[n][:, j : j + 1],
+                    op0=ALU.mult,
+                    op1=ALU.add,
                 )
             z_sb[n] = z_tile
 
@@ -263,7 +265,7 @@ def tile_rotaryembeddingtransformerlayer_pb_t_kernel(
                 for t in range(PACK):
                     nc.tensor.transpose(
                         z_banks[n][t // 2][:, t % 2, j * P : (j + 1) * P],
-                        z_sb[n][:, j, t, :],
+                        z_sb[n][:, j, t : t + D - PACK + 1 : PACK],
                         ident[:],
                     )
 
@@ -356,7 +358,7 @@ def tile_rotaryembeddingtransformerlayer_pb_t_kernel(
             if exists(r - 3):
                 relu_and_store_u(r - 3)
             if exists(r + 1):
-                mean_of_x(r + 1)
+                shift_of_z(r + 1)
             if exists(r - 1):
                 regroup_h(r - 1)
             if exists(r + 4):

@@ -20,9 +20,10 @@ E_PASSES = E // K_PASS
 J = 2
 GROUP = J * P
 N_GROUPS = TOKENS // GROUP
-LOAD_AHEAD = 8
-TR_BANKS = 4
-SECOND_LAYER_ROUND = -3
+FIRST_ROUND = -3
+LOADED_FIRST = 7
+SECOND_LAYER_ROUND = -2
+ATTN_BANKS, Z_BANKS, X_BANKS, U_BANKS = 3, 2, 2, 1
 FLOPS = 2 * TOKENS * (E * D + D * F)
 
 
@@ -48,12 +49,12 @@ def tile_rotaryembeddingtransformerlayer_pb_t_kernel(
     with ExitStack() as ctx:
         ctx.enter_context(tc.manual_schedule())
         const = ctx.enter_context(tc.tile_pool(name="const", bufs=1))
-        loads = ctx.enter_context(tc.tile_pool(name="loads", bufs=5))
+        loads = ctx.enter_context(tc.tile_pool(name="loads", bufs=LOADED_FIRST + 2))
         work = ctx.enter_context(tc.tile_pool(name="work", bufs=2))
-        x_pool = ctx.enter_context(tc.tile_pool(name="x_pool", bufs=5))
+        x_pool = ctx.enter_context(tc.tile_pool(name="x_pool", bufs=6))
         u_pool = ctx.enter_context(tc.tile_pool(name="u_pool", bufs=3))
         stats = ctx.enter_context(tc.tile_pool(name="stats", bufs=4))
-        psum = ctx.enter_context(tc.psum_pool(name="psum", bufs=2))
+        psum = ctx.enter_context(tc.psum_pool(name="psum", bufs=1))
 
         ident = const.tile([P, P], F32)
         make_identity(nc, ident[:])
@@ -79,11 +80,6 @@ def tile_rotaryembeddingtransformerlayer_pb_t_kernel(
         for c in range(D // P):
             nc.sync.dma_start(out=wo_rows[:, c, :], in_=wo_chunks[c])
 
-        bo_bank = psum.tile([P, D], F32, tag="mm1")
-        nc.tensor.matmul(out=bo_bank[:], lhsT=ones[:], rhs=bias_rows[:, 0:D], start=True, stop=True)
-        bo_all = const.tile([P, D], F32)
-        nc.vector.tensor_copy(out=bo_all[:], in_=bo_bank[:])
-
         wo_words = wo_rows[:].bitcast(F32)
         wo_grouped = const.tile([P, E_PASSES, D, PACK], BF16, align_bytes=64)
         wo_grouped_words = wo_grouped[:].bitcast(F32)
@@ -99,14 +95,24 @@ def tile_rotaryembeddingtransformerlayer_pb_t_kernel(
                     in_=wo_grouped[:, g, rows_c, :].rearrange("p d t -> p (d t)"),
                 )
 
-        for c in range(D // P):
-            wo_bank = psum.tile([P, PACK, P], F32, tag="tr", bufs=TR_BANKS)
+        def transpose_wo_chunk(c):
+            wo_bank = psum.tile([P, PACK, P], F32, tag="attn", bufs=ATTN_BANKS)
             transpose_words(nc, wo_bank, wo_words[:, c, :], ident[:])
-            copy_out = nc.vector.tensor_copy if c % 2 == 0 else nc.scalar.copy
+            copy_out = nc.scalar.copy if c % 2 == 0 else nc.vector.tensor_copy
             copy_out(out=wo_grouped_words[:, :, c * P : (c + 1) * P, :], in_=words_side_by_side(wo_bank[:]))
-            if c > 0:
-                quantise_wo_chunk(c - 1)
-        quantise_wo_chunk(D // P - 1)
+
+        bo_all = const.tile([P, D], F32)
+
+        def prepare_first_layer():
+            transpose_wo_chunk(0)
+            transpose_wo_chunk(1)
+            bo_bank = psum.tile([P, D], F32, tag="x", bufs=X_BANKS)
+            nc.tensor.matmul(out=bo_bank[:], lhsT=ones[:], rhs=bias_rows[:, 0:D], start=True, stop=True)
+            nc.vector.tensor_copy(out=bo_all[:], in_=bo_bank[:])
+            for c in range(D // P):
+                quantise_wo_chunk(c)
+                if c + 2 < D // P:
+                    transpose_wo_chunk(c + 2)
 
         b1_all = const.tile([P, F], F32)
         gain_shift = const.tile([P, 2 * PACK], F32)
@@ -114,7 +120,7 @@ def tile_rotaryembeddingtransformerlayer_pb_t_kernel(
         w1_scales = const.tile([P, F], U8, align_bytes=64)
 
         def prepare_second_layer():
-            b1_bank = psum.tile([P, F], F32, tag="mm2")
+            b1_bank = psum.tile([P, F], F32, tag="u", bufs=U_BANKS)
             nc.tensor.matmul(out=b1_bank[:], lhsT=ones[:], rhs=bias_rows[:, D : D + F], start=True, stop=True)
             nc.vector.tensor_copy(out=b1_all[:], in_=b1_bank[:])
 
@@ -123,10 +129,10 @@ def tile_rotaryembeddingtransformerlayer_pb_t_kernel(
 
             w1_words = w1_rows[:].bitcast(F32)
             w1_grouped = const.tile([P, F, PACK], BF16, align_bytes=64)
-            w1_bank = psum.tile([P, F // P, 2, P], F32, tag="tr", bufs=TR_BANKS)
+            w1_bank = psum.tile([P, F // P, 2, P], F32, tag="z", bufs=Z_BANKS)
             for c in range(F // P):
                 transpose_words(nc, w1_bank[:, c], w1_words[:, c, :], ident[:])
-            nc.vector.tensor_copy(
+            nc.scalar.copy(
                 out=w1_grouped[:].bitcast(F32).rearrange("p (c f) u -> p c f u", c=F // P),
                 in_=w1_bank[:].rearrange("p c u f -> p c f u"),
             )
@@ -151,7 +157,7 @@ def tile_rotaryembeddingtransformerlayer_pb_t_kernel(
             attn_words = attn_sb[n][:].bitcast(F32)
             attn_banks[n] = []
             for j in range(J):
-                attn_bank = psum.tile([P, PACK, P], F32, tag="tr", bufs=TR_BANKS)
+                attn_bank = psum.tile([P, PACK, P], F32, tag="attn", bufs=ATTN_BANKS)
                 transpose_words(nc, attn_bank, attn_words[:, j, :], ident[:])
                 attn_banks[n].append(attn_bank)
 
@@ -183,7 +189,7 @@ def tile_rotaryembeddingtransformerlayer_pb_t_kernel(
             codes, scales = attn_mx[n]
             x_banks[n] = []
             for j in range(J):
-                x_bank = psum.tile([P, D], F32, tag="mm1")
+                x_bank = psum.tile([P, D], F32, tag="x", bufs=X_BANKS)
                 for g in range(E_PASSES):
                     nc.tensor.matmul_mx(
                         out=x_bank[:],
@@ -196,19 +202,19 @@ def tile_rotaryembeddingtransformerlayer_pb_t_kernel(
                     )
                 x_banks[n].append(x_bank)
 
-        def finish_x(n, j):
-            if j == 0:
-                sum_tile = stats.tile([P, J], F32)
-                row_sum[n] = sum_tile
-            nc.vector.scalar_tensor_tensor(
-                out=x_sb[n][:, j, :],
-                in0=x_banks[n][j][:],
-                scalar=0.0,
-                in1=x_sb[n][:, j, :],
-                op0=ALU.add,
-                op1=ALU.add,
-                accum_out=row_sum[n][:, j : j + 1],
-            )
+        def finish_x(n):
+            sum_tile = stats.tile([P, J], F32)
+            for j in range(J):
+                nc.vector.scalar_tensor_tensor(
+                    out=x_sb[n][:, j, :],
+                    in0=x_banks[n][j][:],
+                    scalar=0.0,
+                    in1=x_sb[n][:, j, :],
+                    op0=ALU.add,
+                    op1=ALU.add,
+                    accum_out=sum_tile[:, j : j + 1],
+                )
+            row_sum[n] = sum_tile
 
         def store_x(n):
             nc.sync.dma_start(out=x_groups[n], in_=x_sb[n][:])
@@ -259,7 +265,7 @@ def tile_rotaryembeddingtransformerlayer_pb_t_kernel(
         def transpose_z(n):
             z_banks[n] = []
             for half in range(PACK // 2):
-                z_bank = psum.tile([P, 2, GROUP], F32, tag="tr", bufs=TR_BANKS)
+                z_bank = psum.tile([P, 2, GROUP], F32, tag="z", bufs=Z_BANKS)
                 z_banks[n].append(z_bank)
             for j in range(J):
                 for t in range(PACK):
@@ -299,7 +305,7 @@ def tile_rotaryembeddingtransformerlayer_pb_t_kernel(
 
         def second_product(n):
             codes, scales = h_mx[n]
-            u_bank = psum.tile([P, J, F], F32, tag="mm2")
+            u_bank = psum.tile([P, J, F], F32, tag="u", bufs=U_BANKS)
             for j in range(J):
                 nc.tensor.matmul_mx(
                     out=u_bank[:, j, :],
@@ -326,44 +332,32 @@ def tile_rotaryembeddingtransformerlayer_pb_t_kernel(
         def exists(n):
             return 0 <= n < N_GROUPS
 
-        for r in range(-LOAD_AHEAD, N_GROUPS + 3):
-            if exists(r + 4):
-                transpose_attn(r + 4)
-            if exists(r + 1):
-                squared_deviations(r + 1)
-            if exists(r + 2):
-                finish_x(r + 2, 0)
-            if exists(r - 2):
-                quantise_h(r - 2)
-                second_product(r - 2)
-            if exists(r + 3):
-                quantise_attn(r + 3)
-            if exists(r - 3):
-                add_b1(r - 3)
-            if exists(r + 2):
-                finish_x(r + 2, 1)
-                store_x(r + 2)
-            if exists(r + 3):
-                first_product(r + 3)
-            if exists(r):
-                normalise(r)
-            if exists(r + 4):
-                residual(r + 4)
-            if exists(r + 1):
-                invert_std(r + 1)
-            if exists(r - 1):
-                gain_and_shift(r - 1)
-            if exists(r):
-                transpose_z(r)
-            if exists(r - 3):
-                relu_and_store_u(r - 3)
-            if exists(r + 1):
-                shift_of_z(r + 1)
-            if exists(r - 1):
-                regroup_h(r - 1)
-            if exists(r + 4):
-                copy_attn(r + 4)
-            if exists(r + LOAD_AHEAD):
-                load(r + LOAD_AHEAD)
+        def run(stage, n):
+            if exists(n):
+                stage(n)
+
+        for n in range(LOADED_FIRST):
+            load(n)
+        prepare_first_layer()
+        for r in range(FIRST_ROUND, N_GROUPS + 3):
+            run(load, r - FIRST_ROUND + LOADED_FIRST)
+            run(normalise, r - 1)
+            run(gain_and_shift, r - 2)
+            run(transpose_z, r - 1)
+            run(finish_x, r)
+            run(store_x, r)
+            run(add_b1, r - 3)
+            run(regroup_h, r - 2)
+            run(quantise_attn, r + 1)
+            run(quantise_h, r - 2)
+            run(residual, r + 2)
+            run(copy_attn, r + 2)
+            run(transpose_attn, r + 3)
+            run(first_product, r + 1)
+            run(second_product, r - 2)
+            run(relu_and_store_u, r - 3)
+            run(squared_deviations, r)
+            run(invert_std, r)
+            run(shift_of_z, r)
             if r == SECOND_LAYER_ROUND:
                 prepare_second_layer()

@@ -20,9 +20,7 @@ E_PASSES = E // K_PASS
 J = 2
 GROUP = J * P
 N_GROUPS = TOKENS // GROUP
-FIRST_ROUND = -3
-LOADED_FIRST = 7
-SECOND_LAYER_ROUND = -2
+LOADED_FIRST = 6
 ATTN_BANKS, Z_BANKS, X_BANKS, U_BANKS = 3, 2, 2, 1
 FLOPS = 2 * TOKENS * (E * D + D * F)
 
@@ -49,7 +47,7 @@ def tile_rotaryembeddingtransformerlayer_pb_t_kernel(
     with ExitStack() as ctx:
         ctx.enter_context(tc.manual_schedule())
         const = ctx.enter_context(tc.tile_pool(name="const", bufs=1))
-        loads = ctx.enter_context(tc.tile_pool(name="loads", bufs=LOADED_FIRST + 2))
+        loads = ctx.enter_context(tc.tile_pool(name="loads", bufs=LOADED_FIRST + 1))
         work = ctx.enter_context(tc.tile_pool(name="work", bufs=2))
         x_pool = ctx.enter_context(tc.tile_pool(name="x_pool", bufs=6))
         u_pool = ctx.enter_context(tc.tile_pool(name="u_pool", bufs=3))
@@ -61,24 +59,23 @@ def tile_rotaryembeddingtransformerlayer_pb_t_kernel(
         eps_col = const.tile([P, 1], F32)
         nc.vector.memset(eps_col[:], EPS)
 
-        bias_rows = const.tile([P, D + F], BF16)
-        nc.vector.memset(bias_rows[:], 0.0)
-        nc.scalar.dma_start(out=bias_rows[0:1, 0:D], in_=bo.rearrange("(o d) -> o d", o=1))
-        nc.scalar.dma_start(out=bias_rows[0:1, D : D + F], in_=b1.rearrange("(o f) -> o f", o=1))
-        ones = const.tile([P, P], BF16)
-        nc.vector.memset(ones[:], 1.0)
-        gain_bf16 = const.tile([P, PACK], BF16)
-        nc.scalar.dma_start(out=gain_bf16[:], in_=g2.rearrange("(p t) -> p t", t=PACK))
-        shift_bf16 = const.tile([P, PACK], BF16)
-        nc.scalar.dma_start(out=shift_bf16[:], in_=be2.rearrange("(p t) -> p t", t=PACK))
-        w1_rows = const.tile([P, F // P, D], BF16)
-        nc.scalar.dma_start(out=w1_rows[:], in_=W1.rearrange("(c p) d -> p c d", p=P))
-        table_warm = const.tile([P, 1], F32)
-        nc.scalar.activation(out=table_warm[:], in_=eps_col[:], func=ACT.Abs_reciprocal_sqrt)
+        bias_row = const.tile([1, D + F], BF16)
+        nc.sync.dma_start(out=bias_row[:, 0:D], in_=bo.rearrange("(o d) -> o d", o=1))
+        nc.sync.dma_start(out=bias_row[:, D : D + F], in_=b1.rearrange("(o f) -> o f", o=1))
         wo_rows = const.tile([P, D // P, E], BF16)
         wo_chunks = Wo.rearrange("(c p) k -> c p k", p=P)
         for c in range(D // P):
             nc.sync.dma_start(out=wo_rows[:, c, :], in_=wo_chunks[c])
+        ones = const.tile([P, P], BF16)
+        nc.vector.memset(ones[:], 1.0)
+        bias_rows = const.tile([P, D + F], BF16)
+        nc.vector.memset(bias_rows[:], 0.0)
+        gain_bf16 = const.tile([P, PACK], BF16)
+        nc.scalar.dma_start(out=gain_bf16[:], in_=g2.rearrange("(p t) -> p t", t=PACK))
+        shift_bf16 = const.tile([P, PACK], BF16)
+        nc.scalar.dma_start(out=shift_bf16[:], in_=be2.rearrange("(p t) -> p t", t=PACK))
+        table_warm = const.tile([P, 1], F32)
+        nc.scalar.activation(out=table_warm[:], in_=eps_col[:], func=ACT.Abs_reciprocal_sqrt)
 
         wo_words = wo_rows[:].bitcast(F32)
         wo_grouped = const.tile([P, E_PASSES, D, PACK], BF16, align_bytes=64)
@@ -103,39 +100,42 @@ def tile_rotaryembeddingtransformerlayer_pb_t_kernel(
 
         bo_all = const.tile([P, D], F32)
 
-        def prepare_first_layer():
-            transpose_wo_chunk(0)
-            transpose_wo_chunk(1)
+        def spread_bo():
             bo_bank = psum.tile([P, D], F32, tag="x", bufs=X_BANKS)
+            nc.vector.tensor_copy(out=bias_rows[0:1, :], in_=bias_row[:])
             nc.tensor.matmul(out=bo_bank[:], lhsT=ones[:], rhs=bias_rows[:, 0:D], start=True, stop=True)
             nc.vector.tensor_copy(out=bo_all[:], in_=bo_bank[:])
-            for c in range(D // P):
-                quantise_wo_chunk(c)
-                if c + 2 < D // P:
-                    transpose_wo_chunk(c + 2)
 
         b1_all = const.tile([P, F], F32)
         gain_shift = const.tile([P, 2 * PACK], F32)
+        w1_rows = const.tile([P, F // P, D], BF16)
+        w1_grouped = const.tile([P, F, PACK], BF16, align_bytes=64)
         w1_codes = const.tile([P, F], U32, align_bytes=64)
         w1_scales = const.tile([P, F], U8, align_bytes=64)
+        second_layer_banks = {}
 
-        def prepare_second_layer():
+        def load_w1():
+            nc.sync.dma_start(out=w1_rows[:], in_=W1.rearrange("(c p) d -> p c d", p=P))
+
+        def transpose_w1():
             b1_bank = psum.tile([P, F], F32, tag="u", bufs=U_BANKS)
             nc.tensor.matmul(out=b1_bank[:], lhsT=ones[:], rhs=bias_rows[:, D : D + F], start=True, stop=True)
-            nc.vector.tensor_copy(out=b1_all[:], in_=b1_bank[:])
-
-            nc.vector.tensor_copy(out=gain_shift[:, 0:PACK], in_=gain_bf16[:])
-            nc.vector.tensor_copy(out=gain_shift[:, PACK : 2 * PACK], in_=shift_bf16[:])
-
             w1_words = w1_rows[:].bitcast(F32)
-            w1_grouped = const.tile([P, F, PACK], BF16, align_bytes=64)
             w1_bank = psum.tile([P, F // P, 2, P], F32, tag="z", bufs=Z_BANKS)
             for c in range(F // P):
                 transpose_words(nc, w1_bank[:, c], w1_words[:, c, :], ident[:])
+            second_layer_banks["b1"], second_layer_banks["w1"] = b1_bank, w1_bank
+
+        def copy_w1():
+            nc.vector.tensor_copy(out=b1_all[:], in_=second_layer_banks["b1"][:])
+            nc.vector.tensor_copy(out=gain_shift[:, 0:PACK], in_=gain_bf16[:])
+            nc.vector.tensor_copy(out=gain_shift[:, PACK : 2 * PACK], in_=shift_bf16[:])
             nc.scalar.copy(
                 out=w1_grouped[:].bitcast(F32).rearrange("p (c f) u -> p c f u", c=F // P),
-                in_=w1_bank[:].rearrange("p c u f -> p c f u"),
+                in_=second_layer_banks["w1"][:].rearrange("p c u f -> p c f u"),
             )
+
+        def quantise_w1():
             nc.vector.quantize_mx(
                 out=w1_codes[:].bitcast(FP8X4),
                 scales=w1_scales[:],
@@ -338,26 +338,52 @@ def tile_rotaryembeddingtransformerlayer_pb_t_kernel(
 
         for n in range(LOADED_FIRST):
             load(n)
-        prepare_first_layer()
-        for r in range(FIRST_ROUND, N_GROUPS + 3):
-            run(load, r - FIRST_ROUND + LOADED_FIRST)
+            if n == 1:
+                load_w1()
+        spread_bo()
+        for c in range(D // P):
+            transpose_wo_chunk(c)
+            if c == 1:
+                quantise_wo_chunk(0)
+                quantise_wo_chunk(1)
+        transpose_attn(0)
+        quantise_wo_chunk(2)
+        quantise_wo_chunk(3)
+        copy_attn(0)
+        transpose_attn(1)
+        residual(0)
+        quantise_attn(0)
+        first_product(0)
+        copy_attn(1)
+        residual(1)
+        quantise_attn(1)
+        transpose_attn(2)
+        copy_attn(2)
+        transpose_attn(3)
+
+        for r in range(N_GROUPS + 3):
+            run(load, r + LOADED_FIRST)
             run(normalise, r - 1)
             run(gain_and_shift, r - 2)
-            run(transpose_z, r - 1)
             run(finish_x, r)
             run(store_x, r)
+            run(first_product, r + 1)
+            if r == 0:
+                transpose_w1()
+            run(transpose_z, r - 1)
             run(add_b1, r - 3)
             run(regroup_h, r - 2)
-            run(quantise_attn, r + 1)
+            run(quantise_attn, r + 2)
             run(quantise_h, r - 2)
             run(residual, r + 2)
-            run(copy_attn, r + 2)
-            run(transpose_attn, r + 3)
-            run(first_product, r + 1)
+            run(copy_attn, r + 3)
+            run(transpose_attn, r + 4)
             run(second_product, r - 2)
             run(relu_and_store_u, r - 3)
             run(squared_deviations, r)
             run(invert_std, r)
             run(shift_of_z, r)
-            if r == SECOND_LAYER_ROUND:
-                prepare_second_layer()
+            if r == 0:
+                copy_w1()
+            if r == 1:
+                quantise_w1()

@@ -249,18 +249,27 @@ def tile_rotaryembeddingtransformerlayer_pb_t_kernel(
             nc.gpsimd.tensor_tensor(out=shift_tile[:], in0=mean_tile[:], in1=inv_std[n][:], op=ALU.mult)
             shift_z[n] = shift_tile
 
-        def normalise(n):
+        def normalise_tile_0(n):
             z_tile = work.tile([P, J, D], F32)
-            for j in range(J):
-                nc.gpsimd.tensor_scalar(
-                    out=z_tile[:, j, :],
-                    in0=x_sb[n][:, j, :],
-                    scalar1=inv_std[n][:, j : j + 1],
-                    scalar2=shift_z[n][:, j : j + 1],
-                    op0=ALU.mult,
-                    op1=ALU.add,
-                )
+            engine = nc.vector if n == N_GROUPS - 1 else nc.gpsimd
+            engine.tensor_scalar(
+                out=z_tile[:, 0, :],
+                in0=x_sb[n][:, 0, :],
+                scalar1=inv_std[n][:, 0:1],
+                scalar2=shift_z[n][:, 0:1],
+                op0=ALU.mult,
+                op1=ALU.add,
+            )
             z_sb[n] = z_tile
+
+        def normalise_tile_1(n):
+            nc.scalar.activation(
+                out=z_sb[n][:, 1, :],
+                in_=x_sb[n][:, 1, :],
+                func=ACT.Identity,
+                scale=inv_std[n][:, 1:2],
+                bias=shift_z[n][:, 1:2],
+            )
 
         def transpose_z(n):
             z_banks[n] = []
@@ -326,7 +335,10 @@ def tile_rotaryembeddingtransformerlayer_pb_t_kernel(
             u_sb[n] = u_tile
 
         def relu_and_store_u(n):
-            nc.scalar.activation(out=u_sb[n][:], in_=u_sb[n][:], func=ACT.Relu)
+            if n % 2 == 0:
+                nc.scalar.activation(out=u_sb[n][:], in_=u_sb[n][:], func=ACT.Relu)
+            else:
+                nc.vector.tensor_scalar_max(out=u_sb[n][:], in0=u_sb[n][:], scalar1=0.0)
             nc.sync.dma_start(out=u_groups[n], in_=u_sb[n][:])
 
         def exists(n):
@@ -359,30 +371,31 @@ def tile_rotaryembeddingtransformerlayer_pb_t_kernel(
         quantise_attn(1)
         transpose_attn(2)
         copy_attn(2)
-        transpose_attn(3)
 
         for r in range(N_GROUPS + 3):
             run(load, r + LOADED_FIRST)
-            run(normalise, r - 1)
+            run(normalise_tile_0, r - 1)
             run(gain_and_shift, r - 2)
             run(finish_x, r)
             run(store_x, r)
             run(first_product, r + 1)
             if r == 0:
+                transpose_attn(3)
                 transpose_w1()
-            run(transpose_z, r - 1)
             run(add_b1, r - 3)
-            run(regroup_h, r - 2)
             run(quantise_attn, r + 2)
-            run(quantise_h, r - 2)
+            run(regroup_h, r - 2)
             run(residual, r + 2)
+            run(quantise_h, r - 2)
             run(copy_attn, r + 3)
+            run(normalise_tile_1, r - 1)
             run(transpose_attn, r + 4)
+            run(transpose_z, r - 1)
             run(second_product, r - 2)
-            run(relu_and_store_u, r - 3)
             run(squared_deviations, r)
             run(invert_std, r)
             run(shift_of_z, r)
+            run(relu_and_store_u, r - 3)
             if r == 0:
                 copy_w1()
             if r == 1:

@@ -21,6 +21,7 @@ J = 2
 GROUP = J * P
 N_GROUPS = TOKENS // GROUP
 LOADED_FIRST = 6
+WARM_UP = 3
 ATTN_BANKS, Z_BANKS, X_BANKS, U_BANKS = 3, 2, 2, 1
 FLOPS = 2 * TOKENS * (E * D + D * F)
 
@@ -56,6 +57,8 @@ def tile_rotaryembeddingtransformerlayer_pb_t_kernel(
 
         ident = const.tile([P, P], F32)
         make_identity(nc, ident[:])
+        ones = const.tile([P, D], BF16)
+        nc.vector.memset(ones[:], 1.0)
         eps_col = const.tile([P, 1], F32)
         nc.vector.memset(eps_col[:], EPS)
 
@@ -66,48 +69,59 @@ def tile_rotaryembeddingtransformerlayer_pb_t_kernel(
         wo_chunks = Wo.rearrange("(c p) k -> c p k", p=P)
         for c in range(D // P):
             nc.sync.dma_start(out=wo_rows[:, c, :], in_=wo_chunks[c])
-        ones = const.tile([P, P], BF16)
-        nc.vector.memset(ones[:], 1.0)
         bias_rows = const.tile([P, D + F], BF16)
         nc.vector.memset(bias_rows[:], 0.0)
         gain_bf16 = const.tile([P, PACK], BF16)
         nc.scalar.dma_start(out=gain_bf16[:], in_=g2.rearrange("(p t) -> p t", t=PACK))
         shift_bf16 = const.tile([P, PACK], BF16)
         nc.scalar.dma_start(out=shift_bf16[:], in_=be2.rearrange("(p t) -> p t", t=PACK))
+        gain_shift = const.tile([P, 2 * PACK], F32)
+        nc.gpsimd.tensor_copy(out=gain_shift[:, 0:PACK], in_=gain_bf16[:])
+        nc.gpsimd.tensor_copy(out=gain_shift[:, PACK : 2 * PACK], in_=shift_bf16[:])
         table_warm = const.tile([P, 1], F32)
         nc.scalar.activation(out=table_warm[:], in_=eps_col[:], func=ACT.Abs_reciprocal_sqrt)
 
         wo_words = wo_rows[:].bitcast(F32)
-        wo_grouped = const.tile([P, E_PASSES, D, PACK], BF16, align_bytes=64)
-        wo_grouped_words = wo_grouped[:].bitcast(F32)
+        wo_grouped = []
+        for half in range(2):
+            half_tile = const.tile([P, E_PASSES, D // 2, PACK], BF16, align_bytes=64, name=f"wo_grouped_{half}")
+            wo_grouped.append(half_tile)
         wo_codes = const.tile([P, E_PASSES, D], U32, align_bytes=64)
         wo_scales = const.tile([P, E_PASSES, D], U8, align_bytes=64)
 
-        def quantise_wo_chunk(c):
-            rows_c = slice(c * P, (c + 1) * P)
+        def quantise_wo(half):
+            rows = slice(half * (D // 2), (half + 1) * (D // 2))
             for g in range(E_PASSES):
                 nc.vector.quantize_mx(
-                    out=wo_codes[:, g, rows_c].bitcast(FP8X4),
-                    scales=wo_scales[:, g, rows_c],
-                    in_=wo_grouped[:, g, rows_c, :].rearrange("p d t -> p (d t)"),
+                    out=wo_codes[:, g, rows].bitcast(FP8X4),
+                    scales=wo_scales[:, g, rows],
+                    in_=wo_grouped[half][:, g].rearrange("p d t -> p (d t)"),
                 )
 
         def transpose_wo_chunk(c):
             wo_bank = psum.tile([P, PACK, P], F32, tag="attn", bufs=ATTN_BANKS)
             transpose_words(nc, wo_bank, wo_words[:, c, :], ident[:])
-            copy_out = nc.scalar.copy if c % 2 == 0 else nc.vector.tensor_copy
-            copy_out(out=wo_grouped_words[:, :, c * P : (c + 1) * P, :], in_=words_side_by_side(wo_bank[:]))
+            copy_out = nc.vector.tensor_copy if c == 1 else nc.scalar.copy
+            half, place = divmod(c, 2)
+            grouped_words = wo_grouped[half][:].bitcast(F32)
+            copy_out(
+                out=grouped_words[:, :, place * P : (place + 1) * P, :], in_=words_side_by_side(wo_bank[:])
+            )
 
         bo_all = const.tile([P, D], F32)
+
+        def keep_warm():
+            idle_bank = psum.tile([P, D], F32, tag="u", bufs=U_BANKS)
+            for _ in range(WARM_UP):
+                nc.tensor.matmul(out=idle_bank[:], lhsT=ones[:, 0:P], rhs=ones[:], start=True, stop=True)
 
         def spread_bo():
             bo_bank = psum.tile([P, D], F32, tag="x", bufs=X_BANKS)
             nc.vector.tensor_copy(out=bias_rows[0:1, :], in_=bias_row[:])
-            nc.tensor.matmul(out=bo_bank[:], lhsT=ones[:], rhs=bias_rows[:, 0:D], start=True, stop=True)
+            nc.tensor.matmul(out=bo_bank[:], lhsT=ones[:, 0:P], rhs=bias_rows[:, 0:D], start=True, stop=True)
             nc.vector.tensor_copy(out=bo_all[:], in_=bo_bank[:])
 
         b1_all = const.tile([P, F], F32)
-        gain_shift = const.tile([P, 2 * PACK], F32)
         w1_rows = const.tile([P, F // P, D], BF16)
         w1_grouped = const.tile([P, F, PACK], BF16, align_bytes=64)
         w1_codes = const.tile([P, F], U32, align_bytes=64)
@@ -119,7 +133,7 @@ def tile_rotaryembeddingtransformerlayer_pb_t_kernel(
 
         def transpose_w1():
             b1_bank = psum.tile([P, F], F32, tag="u", bufs=U_BANKS)
-            nc.tensor.matmul(out=b1_bank[:], lhsT=ones[:], rhs=bias_rows[:, D : D + F], start=True, stop=True)
+            nc.tensor.matmul(out=b1_bank[:], lhsT=ones[:, 0:P], rhs=bias_rows[:, D : D + F], start=True, stop=True)
             w1_words = w1_rows[:].bitcast(F32)
             w1_bank = psum.tile([P, F // P, 2, P], F32, tag="z", bufs=Z_BANKS)
             for c in range(F // P):
@@ -127,9 +141,7 @@ def tile_rotaryembeddingtransformerlayer_pb_t_kernel(
             second_layer_banks["b1"], second_layer_banks["w1"] = b1_bank, w1_bank
 
         def copy_w1():
-            nc.vector.tensor_copy(out=b1_all[:], in_=second_layer_banks["b1"][:])
-            nc.vector.tensor_copy(out=gain_shift[:, 0:PACK], in_=gain_bf16[:])
-            nc.vector.tensor_copy(out=gain_shift[:, PACK : 2 * PACK], in_=shift_bf16[:])
+            nc.scalar.copy(out=b1_all[:], in_=second_layer_banks["b1"][:])
             nc.scalar.copy(
                 out=w1_grouped[:].bitcast(F32).rearrange("p (c f) u -> p c f u", c=F // P),
                 in_=second_layer_banks["w1"][:].rearrange("p c u f -> p c f u"),
@@ -241,13 +253,23 @@ def tile_rotaryembeddingtransformerlayer_pb_t_kernel(
             inv_std[n] = inv_tile
 
         def shift_of_z(n):
+            shift_tile = stats.tile([P, J], F32)
+            shift_z[n] = shift_tile
+            if n == N_GROUPS - 1:
+                nc.vector.scalar_tensor_tensor(
+                    out=shift_tile[:],
+                    in0=row_sum[n][:],
+                    scalar=-1.0 / D,
+                    in1=inv_std[n][:],
+                    op0=ALU.mult,
+                    op1=ALU.mult,
+                )
+                return
             mean_tile = stats.tile([P, J], F32)
             nc.gpsimd.tensor_scalar(
                 out=mean_tile[:], in0=row_sum[n][:], scalar1=-1.0 / D, scalar2=0.0, op0=ALU.mult, op1=ALU.add
             )
-            shift_tile = stats.tile([P, J], F32)
             nc.gpsimd.tensor_tensor(out=shift_tile[:], in0=mean_tile[:], in1=inv_std[n][:], op=ALU.mult)
-            shift_z[n] = shift_tile
 
         def normalise_tile_0(n):
             z_tile = work.tile([P, J, D], F32)
@@ -352,19 +374,19 @@ def tile_rotaryembeddingtransformerlayer_pb_t_kernel(
             load(n)
             if n == 1:
                 load_w1()
+        keep_warm()
         spread_bo()
         for c in range(D // P):
             transpose_wo_chunk(c)
             if c == 1:
-                quantise_wo_chunk(0)
-                quantise_wo_chunk(1)
+                quantise_wo(0)
         transpose_attn(0)
-        quantise_wo_chunk(2)
-        quantise_wo_chunk(3)
+        quantise_wo(1)
         copy_attn(0)
         transpose_attn(1)
         residual(0)
         quantise_attn(0)
+        keep_warm()
         first_product(0)
         copy_attn(1)
         residual(1)

@@ -22,6 +22,7 @@ GROUP = J * P
 N_GROUPS = TOKENS // GROUP
 LOADED_FIRST = 6
 WARM_UP = 3
+VECTOR_SHARES_COPY = (3, 4)
 ATTN_BANKS, Z_BANKS, X_BANKS, U_BANKS = 3, 2, 2, 1
 FLOPS = 2 * TOKENS * (E * D + D * F)
 
@@ -177,7 +178,8 @@ def tile_rotaryembeddingtransformerlayer_pb_t_kernel(
             attn_side = work.tile([P, J, E_PASSES, P, PACK], BF16, align_bytes=64)
             attn_side_words = attn_side[:].bitcast(F32)
             for j in range(J):
-                nc.scalar.copy(out=attn_side_words[:, j, :, :, :], in_=words_side_by_side(attn_banks[n][j][:]))
+                copy_out = nc.vector.tensor_copy if n in VECTOR_SHARES_COPY and j == 1 else nc.scalar.copy
+                copy_out(out=attn_side_words[:, j, :, :, :], in_=words_side_by_side(attn_banks[n][j][:]))
             attn_grouped[n] = attn_side
 
         def quantise_attn(n):
@@ -271,27 +273,30 @@ def tile_rotaryembeddingtransformerlayer_pb_t_kernel(
             )
             nc.gpsimd.tensor_tensor(out=shift_tile[:], in0=mean_tile[:], in1=inv_std[n][:], op=ALU.mult)
 
-        def normalise_tile_0(n):
+        def normalise_early(n):
             z_tile = work.tile([P, J, D], F32)
-            engine = nc.vector if n == N_GROUPS - 1 else nc.gpsimd
-            engine.tensor_scalar(
-                out=z_tile[:, 0, :],
-                in0=x_sb[n][:, 0, :],
-                scalar1=inv_std[n][:, 0:1],
-                scalar2=shift_z[n][:, 0:1],
-                op0=ALU.mult,
-                op1=ALU.add,
-            )
             z_sb[n] = z_tile
+            draining = n >= N_GROUPS - 2
+            engine = nc.vector if draining else nc.gpsimd
+            for j in range(J if draining else 1):
+                engine.tensor_scalar(
+                    out=z_tile[:, j, :],
+                    in0=x_sb[n][:, j, :],
+                    scalar1=inv_std[n][:, j : j + 1],
+                    scalar2=shift_z[n][:, j : j + 1],
+                    op0=ALU.mult,
+                    op1=ALU.add,
+                )
 
-        def normalise_tile_1(n):
-            nc.scalar.activation(
-                out=z_sb[n][:, 1, :],
-                in_=x_sb[n][:, 1, :],
-                func=ACT.Identity,
-                scale=inv_std[n][:, 1:2],
-                bias=shift_z[n][:, 1:2],
-            )
+        def normalise_late(n):
+            if n < N_GROUPS - 2:
+                nc.scalar.activation(
+                    out=z_sb[n][:, 1, :],
+                    in_=x_sb[n][:, 1, :],
+                    func=ACT.Identity,
+                    scale=inv_std[n][:, 1:2],
+                    bias=shift_z[n][:, 1:2],
+                )
 
         def transpose_z(n):
             z_banks[n] = []
@@ -309,13 +314,15 @@ def tile_rotaryembeddingtransformerlayer_pb_t_kernel(
         def gain_and_shift(n):
             planes = work.tile([P, PACK, GROUP], BF16)
             for t in range(PACK):
-                nc.scalar.activation(
-                    out=planes[:, t, :],
-                    in_=z_banks[n][t // 2][:, t % 2, :],
-                    func=ACT.Identity,
-                    scale=gain_shift[:, t : t + 1],
-                    bias=gain_shift[:, PACK + t : PACK + t + 1],
-                )
+                z_plane = z_banks[n][t // 2][:, t % 2, :]
+                gain = gain_shift[:, t : t + 1]
+                shift = gain_shift[:, PACK + t : PACK + t + 1]
+                if n == N_GROUPS - 1 and t >= PACK // 2:
+                    nc.vector.tensor_scalar(
+                        out=planes[:, t, :], in0=z_plane, scalar1=gain, scalar2=shift, op0=ALU.mult, op1=ALU.add
+                    )
+                else:
+                    nc.scalar.activation(out=planes[:, t, :], in_=z_plane, func=ACT.Identity, scale=gain, bias=shift)
             h_planes[n] = planes
 
         def regroup_h(n):
@@ -396,11 +403,11 @@ def tile_rotaryembeddingtransformerlayer_pb_t_kernel(
 
         for r in range(N_GROUPS + 3):
             run(load, r + LOADED_FIRST)
-            run(normalise_tile_0, r - 1)
             run(gain_and_shift, r - 2)
             run(finish_x, r)
             run(store_x, r)
             run(first_product, r + 1)
+            run(normalise_early, r - 1)
             if r == 0:
                 transpose_attn(3)
                 transpose_w1()
@@ -410,7 +417,7 @@ def tile_rotaryembeddingtransformerlayer_pb_t_kernel(
             run(residual, r + 2)
             run(quantise_h, r - 2)
             run(copy_attn, r + 3)
-            run(normalise_tile_1, r - 1)
+            run(normalise_late, r - 1)
             run(transpose_attn, r + 4)
             run(transpose_z, r - 1)
             run(second_product, r - 2)

@@ -17,9 +17,8 @@ K_PASS = P * PACK
 TOKENS, E, D, F = 4096, 1024, 512, 256
 EPS = 1e-5
 E_PASSES = E // K_PASS
-J = 2
-GROUP = J * P
-N_GROUPS = TOKENS // GROUP
+GROUP_TILES = [2] * (TOKENS // P // 2 - 1) + [1, 1]
+N_GROUPS = len(GROUP_TILES)
 LOADED_FIRST = 6
 WARM_UP = 3
 VECTOR_SHARES_COPY = (3, 4)
@@ -41,10 +40,14 @@ def tile_rotaryembeddingtransformerlayer_pb_t_kernel(
     tc, attn, src_norm, Wo, bo, g2, be2, W1, b1, out_0, out_1
 ):
     nc = tc.nc
-    attn_groups = attn.flatten_outer_dims().rearrange("(n p j) k -> n p j k", p=P, j=J)
-    src_groups = src_norm.flatten_outer_dims().rearrange("(n p j) d -> n p j d", p=P, j=J)
-    x_groups = out_0.flatten_outer_dims().rearrange("(n p j) d -> n p j d", p=P, j=J)
-    u_groups = out_1.flatten_outer_dims().rearrange("(n p j) f -> n p j f", p=P, j=J)
+    attn_tokens = attn.flatten_outer_dims()
+    src_tokens = src_norm.flatten_outer_dims()
+    x_tokens = out_0.flatten_outer_dims()
+    u_tokens = out_1.flatten_outer_dims()
+
+    def group_rows(tokens, n):
+        first = P * sum(GROUP_TILES[:n])
+        return tokens[first : first + P * GROUP_TILES[n], :].rearrange("(p j) c -> p j c", j=GROUP_TILES[n])
 
     with ExitStack() as ctx:
         ctx.enter_context(tc.manual_schedule())
@@ -157,16 +160,18 @@ def tile_rotaryembeddingtransformerlayer_pb_t_kernel(
 
         attn_sb, src_sb, attn_banks, attn_grouped, attn_mx = {}, {}, {}, {}, {}
         x_sb, x_banks, row_sum, sum_sq, inv_std, shift_z = {}, {}, {}, {}, {}, {}
-        z_sb, z_banks, h_planes, h_grouped, h_mx, u_banks, u_sb = {}, {}, {}, {}, {}, {}, {}
+        z_sb, z_planes, h_planes, h_grouped, h_mx, u_banks, u_sb = {}, {}, {}, {}, {}, {}, {}
 
         def load(n):
+            J = GROUP_TILES[n]
             attn_tile = loads.tile([P, J, E], BF16)
-            nc.sync.dma_start(out=attn_tile[:], in_=attn_groups[n])
+            nc.sync.dma_start(out=attn_tile[:], in_=group_rows(attn_tokens, n))
             src_tile = loads.tile([P, J, D], BF16)
-            nc.sync.dma_start(out=src_tile[:], in_=src_groups[n])
+            nc.sync.dma_start(out=src_tile[:], in_=group_rows(src_tokens, n))
             attn_sb[n], src_sb[n] = attn_tile, src_tile
 
         def transpose_attn(n):
+            J = GROUP_TILES[n]
             attn_words = attn_sb[n][:].bitcast(F32)
             attn_banks[n] = []
             for j in range(J):
@@ -175,6 +180,7 @@ def tile_rotaryembeddingtransformerlayer_pb_t_kernel(
                 attn_banks[n].append(attn_bank)
 
         def copy_attn(n):
+            J = GROUP_TILES[n]
             attn_side = work.tile([P, J, E_PASSES, P, PACK], BF16, align_bytes=64)
             attn_side_words = attn_side[:].bitcast(F32)
             for j in range(J):
@@ -183,6 +189,7 @@ def tile_rotaryembeddingtransformerlayer_pb_t_kernel(
             attn_grouped[n] = attn_side
 
         def quantise_attn(n):
+            J = GROUP_TILES[n]
             attn_codes = work.tile([P, J, E_PASSES, P], U32, align_bytes=64)
             attn_scales = work.tile([P, J, E_PASSES, P], U8, align_bytes=64)
             nc.vector.quantize_mx(
@@ -193,6 +200,7 @@ def tile_rotaryembeddingtransformerlayer_pb_t_kernel(
             attn_mx[n] = (attn_codes, attn_scales)
 
         def residual(n):
+            J = GROUP_TILES[n]
             x_tile = x_pool.tile([P, J, D], F32)
             nc.vector.tensor_tensor(
                 out=x_tile[:], in0=src_sb[n][:], in1=bo_all[:].unsqueeze(1).to_broadcast([P, J, D]), op=ALU.add
@@ -200,6 +208,7 @@ def tile_rotaryembeddingtransformerlayer_pb_t_kernel(
             x_sb[n] = x_tile
 
         def first_product(n):
+            J = GROUP_TILES[n]
             codes, scales = attn_mx[n]
             x_banks[n] = []
             for j in range(J):
@@ -217,6 +226,7 @@ def tile_rotaryembeddingtransformerlayer_pb_t_kernel(
                 x_banks[n].append(x_bank)
 
         def finish_x(n):
+            J = GROUP_TILES[n]
             sum_tile = stats.tile([P, J], F32)
             for j in range(J):
                 nc.vector.scalar_tensor_tensor(
@@ -231,9 +241,10 @@ def tile_rotaryembeddingtransformerlayer_pb_t_kernel(
             row_sum[n] = sum_tile
 
         def store_x(n):
-            nc.sync.dma_start(out=x_groups[n], in_=x_sb[n][:])
+            nc.sync.dma_start(out=group_rows(x_tokens, n), in_=x_sb[n][:])
 
         def squared_deviations(n):
+            J = GROUP_TILES[n]
             squares = work.tile([P, J, D], BF16)
             sq_tile = stats.tile([P, J], F32)
             for j in range(J):
@@ -248,6 +259,7 @@ def tile_rotaryembeddingtransformerlayer_pb_t_kernel(
             sum_sq[n] = sq_tile
 
         def invert_std(n):
+            J = GROUP_TILES[n]
             inv_tile = stats.tile([P, J], F32)
             nc.scalar.activation(
                 out=inv_tile[:], in_=sum_sq[n][:], func=ACT.Abs_reciprocal_sqrt, scale=1.0 / D**3, bias=eps_col[:]
@@ -255,6 +267,7 @@ def tile_rotaryembeddingtransformerlayer_pb_t_kernel(
             inv_std[n] = inv_tile
 
         def shift_of_z(n):
+            J = GROUP_TILES[n]
             shift_tile = stats.tile([P, J], F32)
             shift_z[n] = shift_tile
             if n == N_GROUPS - 1:
@@ -274,6 +287,7 @@ def tile_rotaryembeddingtransformerlayer_pb_t_kernel(
             nc.gpsimd.tensor_tensor(out=shift_tile[:], in0=mean_tile[:], in1=inv_std[n][:], op=ALU.mult)
 
         def normalise_early(n):
+            J = GROUP_TILES[n]
             z_tile = work.tile([P, J, D], F32)
             z_sb[n] = z_tile
             draining = n >= N_GROUPS - 2
@@ -299,34 +313,36 @@ def tile_rotaryembeddingtransformerlayer_pb_t_kernel(
                 )
 
         def transpose_z(n):
-            z_banks[n] = []
-            for half in range(PACK // 2):
-                z_bank = psum.tile([P, 2, GROUP], F32, tag="z", bufs=Z_BANKS)
-                z_banks[n].append(z_bank)
+            J = GROUP_TILES[n]
+            banks = []
+            for b in range(J):
+                z_bank = psum.tile([P, PACK // J, J * P], F32, tag="z", bufs=Z_BANKS)
+                banks.append(z_bank)
+            z_planes[n] = [banks[t * J // PACK][:, t % (PACK // J), :] for t in range(PACK)]
             for j in range(J):
                 for t in range(PACK):
                     nc.tensor.transpose(
-                        z_banks[n][t // 2][:, t % 2, j * P : (j + 1) * P],
+                        z_planes[n][t][:, j * P : (j + 1) * P],
                         z_sb[n][:, j, t : t + D - PACK + 1 : PACK],
                         ident[:],
                     )
 
         def gain_and_shift(n):
-            planes = work.tile([P, PACK, GROUP], BF16)
+            J = GROUP_TILES[n]
+            planes = work.tile([P, PACK, J * P], BF16)
             for t in range(PACK):
-                z_plane = z_banks[n][t // 2][:, t % 2, :]
-                gain = gain_shift[:, t : t + 1]
-                shift = gain_shift[:, PACK + t : PACK + t + 1]
-                if n == N_GROUPS - 1 and t >= PACK // 2:
-                    nc.vector.tensor_scalar(
-                        out=planes[:, t, :], in0=z_plane, scalar1=gain, scalar2=shift, op0=ALU.mult, op1=ALU.add
-                    )
-                else:
-                    nc.scalar.activation(out=planes[:, t, :], in_=z_plane, func=ACT.Identity, scale=gain, bias=shift)
+                nc.scalar.activation(
+                    out=planes[:, t, :],
+                    in_=z_planes[n][t],
+                    func=ACT.Identity,
+                    scale=gain_shift[:, t : t + 1],
+                    bias=gain_shift[:, PACK + t : PACK + t + 1],
+                )
             h_planes[n] = planes
 
         def regroup_h(n):
-            h_side = work.tile([P, GROUP, PACK], BF16, align_bytes=64)
+            J = GROUP_TILES[n]
+            h_side = work.tile([P, J * P, PACK], BF16, align_bytes=64)
             nc.vector.tensor_copy(
                 out=h_side[:].rearrange("p (c i) t -> p c t i", i=4),
                 in_=h_planes[n][:].rearrange("p t (c i) -> p c t i", i=4),
@@ -334,14 +350,16 @@ def tile_rotaryembeddingtransformerlayer_pb_t_kernel(
             h_grouped[n] = h_side
 
         def quantise_h(n):
-            h_codes = work.tile([P, GROUP], U32, align_bytes=64)
-            h_scales = work.tile([P, GROUP], U8, align_bytes=64)
+            J = GROUP_TILES[n]
+            h_codes = work.tile([P, J * P], U32, align_bytes=64)
+            h_scales = work.tile([P, J * P], U8, align_bytes=64)
             nc.vector.quantize_mx(
                 out=h_codes[:].bitcast(FP8X4), scales=h_scales[:], in_=h_grouped[n][:].rearrange("p k t -> p (k t)")
             )
             h_mx[n] = (h_codes, h_scales)
 
         def second_product(n):
+            J = GROUP_TILES[n]
             codes, scales = h_mx[n]
             u_bank = psum.tile([P, J, F], F32, tag="u", bufs=U_BANKS)
             for j in range(J):
@@ -357,6 +375,7 @@ def tile_rotaryembeddingtransformerlayer_pb_t_kernel(
             u_banks[n] = u_bank
 
         def add_b1(n):
+            J = GROUP_TILES[n]
             u_tile = u_pool.tile([P, J, F], F32)
             nc.vector.tensor_tensor(
                 out=u_tile[:], in0=u_banks[n][:], in1=b1_all[:].unsqueeze(1).to_broadcast([P, J, F]), op=ALU.add
@@ -364,11 +383,11 @@ def tile_rotaryembeddingtransformerlayer_pb_t_kernel(
             u_sb[n] = u_tile
 
         def relu_and_store_u(n):
-            if n % 2 == 0:
+            if n % 2 == 0 and n < N_GROUPS - 1:
                 nc.scalar.activation(out=u_sb[n][:], in_=u_sb[n][:], func=ACT.Relu)
             else:
                 nc.vector.tensor_scalar_max(out=u_sb[n][:], in0=u_sb[n][:], scalar1=0.0)
-            nc.sync.dma_start(out=u_groups[n], in_=u_sb[n][:])
+            nc.sync.dma_start(out=group_rows(u_tokens, n), in_=u_sb[n][:])
 
         def exists(n):
             return 0 <= n < N_GROUPS

@@ -12,6 +12,7 @@ ALU = mybir.AluOpType
 ACT = mybir.ActivationFunctionType
 
 P = 128
+RUN = 8
 PACK = 4
 K_PASS = P * PACK
 TOKENS, E, D, F = 4096, 1024, 512, 256
@@ -30,6 +31,10 @@ def transpose_words(nc, bank, rows, ident):
     for b in range(rows.shape[1] // P):
         first = (b // 2) * 2 * P + b % 2
         nc.tensor.transpose(bank[:, b, :], rows[:, first : first + 2 * P - 1 : 2], ident)
+
+
+def in_runs(rows):
+    return rows.rearrange("p (q t i) -> p t q i", t=PACK, i=RUN)
 
 
 def words_side_by_side(bank):
@@ -75,13 +80,9 @@ def tile_rotaryembeddingtransformerlayer_pb_t_kernel(
             nc.sync.dma_start(out=wo_rows[:, c, :], in_=wo_chunks[c])
         bias_rows = const.tile([P, D + F], BF16)
         nc.vector.memset(bias_rows[:], 0.0)
-        gain_bf16 = const.tile([P, PACK], BF16)
-        nc.scalar.dma_start(out=gain_bf16[:], in_=g2.rearrange("(p t) -> p t", t=PACK))
-        shift_bf16 = const.tile([P, PACK], BF16)
-        nc.scalar.dma_start(out=shift_bf16[:], in_=be2.rearrange("(p t) -> p t", t=PACK))
+        norm_rows = const.tile([P, P], BF16)
+        nc.gpsimd.memset(norm_rows[:], 0.0)
         gain_shift = const.tile([P, 2 * PACK], F32)
-        nc.gpsimd.tensor_copy(out=gain_shift[:, 0:PACK], in_=gain_bf16[:])
-        nc.gpsimd.tensor_copy(out=gain_shift[:, PACK : 2 * PACK], in_=shift_bf16[:])
         table_warm = const.tile([P, 1], F32)
         nc.scalar.activation(out=table_warm[:], in_=eps_col[:], func=ACT.Abs_reciprocal_sqrt)
 
@@ -127,29 +128,49 @@ def tile_rotaryembeddingtransformerlayer_pb_t_kernel(
 
         b1_all = const.tile([P, F], F32)
         w1_rows = const.tile([P, F // P, D], BF16)
+        w1_f32 = const.tile([P, F // P, PACK, P], F32)
+        norm_rows_f32 = const.tile([P, P], F32)
         w1_grouped = const.tile([P, F, PACK], BF16, align_bytes=64)
         w1_codes = const.tile([P, F], U32, align_bytes=64)
         w1_scales = const.tile([P, F], U8, align_bytes=64)
         second_layer_banks = {}
 
-        def load_w1():
+        def load_second_layer():
+            for first_row, vector in ((0, g2), (PACK, be2)):
+                nc.sync.dma_start(
+                    out=norm_rows[first_row : first_row + PACK, :].rearrange("t (q i) -> t q i", i=RUN),
+                    in_=vector.rearrange("(q t i) -> t q i", t=PACK, i=RUN),
+                )
             nc.sync.dma_start(out=w1_rows[:], in_=W1.rearrange("(c p) d -> p c d", p=P))
 
-        def transpose_w1():
-            b1_bank = psum.tile([P, F], F32, tag="u", bufs=U_BANKS)
-            nc.tensor.matmul(out=b1_bank[:], lhsT=ones[:, 0:P], rhs=bias_rows[:, D : D + F], start=True, stop=True)
-            w1_words = w1_rows[:].bitcast(F32)
-            w1_bank = psum.tile([P, F // P, 2, P], F32, tag="z", bufs=Z_BANKS)
+        def widen_w1():
             for c in range(F // P):
-                transpose_words(nc, w1_bank[:, c], w1_words[:, c, :], ident[:])
-            second_layer_banks["b1"], second_layer_banks["w1"] = b1_bank, w1_bank
+                nc.scalar.copy(out=w1_f32[:, c].rearrange("p t (q i) -> p t q i", i=RUN), in_=in_runs(w1_rows[:, c, :]))
+            nc.scalar.copy(out=norm_rows_f32[:], in_=norm_rows[:])
+
+        def transpose_w1():
+            vectors_bank = psum.tile([P, F + P], F32, tag="u", bufs=U_BANKS)
+            nc.tensor.transpose(vectors_bank[:, F : F + P], norm_rows_f32[:], ident[:])
+            w1_banks = []
+            for c in range(F // P):
+                w1_bank = psum.tile([P, PACK, P], F32, tag="z", bufs=Z_BANKS)
+                for t in range(PACK):
+                    nc.tensor.transpose(w1_bank[:, t, :], w1_f32[:, c, t, :], ident[:])
+                w1_banks.append(w1_bank)
+            nc.tensor.matmul(
+                out=vectors_bank[:, 0:F], lhsT=ones[:, 0:P], rhs=bias_rows[:, D : D + F], start=True, stop=True
+            )
+            second_layer_banks["vectors"], second_layer_banks["w1"] = vectors_bank, w1_banks
 
         def copy_w1():
-            nc.scalar.copy(out=b1_all[:], in_=second_layer_banks["b1"][:])
-            nc.scalar.copy(
-                out=w1_grouped[:].bitcast(F32).rearrange("p (c f) u -> p c f u", c=F // P),
-                in_=second_layer_banks["w1"][:].rearrange("p c u f -> p c f u"),
-            )
+            vectors_bank = second_layer_banks["vectors"]
+            nc.scalar.copy(out=b1_all[:], in_=vectors_bank[:, 0:F])
+            nc.scalar.copy(out=gain_shift[:], in_=vectors_bank[:, F : F + 2 * PACK])
+            for c in range(F // P):
+                nc.scalar.copy(
+                    out=w1_grouped[:, c * P : (c + 1) * P, :],
+                    in_=second_layer_banks["w1"][c][:].rearrange("p t f -> p f t"),
+                )
 
         def quantise_w1():
             nc.vector.quantize_mx(
@@ -286,16 +307,19 @@ def tile_rotaryembeddingtransformerlayer_pb_t_kernel(
             )
             nc.gpsimd.tensor_tensor(out=shift_tile[:], in0=mean_tile[:], in1=inv_std[n][:], op=ALU.mult)
 
+        def z_in_runs(z_tile, j):
+            return z_tile[:, j].rearrange("p t (q i) -> p t q i", i=RUN)
+
         def normalise_early(n):
             J = GROUP_TILES[n]
-            z_tile = work.tile([P, J, D], F32)
+            z_tile = work.tile([P, J, PACK, P], F32)
             z_sb[n] = z_tile
             draining = n >= N_GROUPS - 2
             engine = nc.vector if draining else nc.gpsimd
             for j in range(J if draining else 1):
                 engine.tensor_scalar(
-                    out=z_tile[:, j, :],
-                    in0=x_sb[n][:, j, :],
+                    out=z_in_runs(z_tile, j),
+                    in0=in_runs(x_sb[n][:, j, :]),
                     scalar1=inv_std[n][:, j : j + 1],
                     scalar2=shift_z[n][:, j : j + 1],
                     op0=ALU.mult,
@@ -305,8 +329,8 @@ def tile_rotaryembeddingtransformerlayer_pb_t_kernel(
         def normalise_late(n):
             if n < N_GROUPS - 2:
                 nc.scalar.activation(
-                    out=z_sb[n][:, 1, :],
-                    in_=x_sb[n][:, 1, :],
+                    out=z_in_runs(z_sb[n], 1),
+                    in_=in_runs(x_sb[n][:, 1, :]),
                     func=ACT.Identity,
                     scale=inv_std[n][:, 1:2],
                     bias=shift_z[n][:, 1:2],
@@ -323,7 +347,7 @@ def tile_rotaryembeddingtransformerlayer_pb_t_kernel(
                 for t in range(PACK):
                     nc.tensor.transpose(
                         z_planes[n][t][:, j * P : (j + 1) * P],
-                        z_sb[n][:, j, t : t + D - PACK + 1 : PACK],
+                        z_sb[n][:, j, t, :],
                         ident[:],
                     )
 
@@ -399,7 +423,7 @@ def tile_rotaryembeddingtransformerlayer_pb_t_kernel(
         for n in range(LOADED_FIRST):
             load(n)
             if n == 1:
-                load_w1()
+                load_second_layer()
         keep_warm()
         spread_bo()
         for c in range(D // P):
@@ -415,6 +439,7 @@ def tile_rotaryembeddingtransformerlayer_pb_t_kernel(
         keep_warm()
         first_product(0)
         copy_attn(1)
+        widen_w1()
         residual(1)
         quantise_attn(1)
         transpose_attn(2)

from contextlib import ExitStack

import concourse.mybir as mybir
from concourse.masks import make_identity

F32 = mybir.dt.float32
BF16 = mybir.dt.bfloat16
U32 = mybir.dt.uint32
U8 = mybir.dt.uint8
FP8X4 = mybir.dt.float8_e4m3fn_x4
ALU = mybir.AluOpType
ACT = mybir.ActivationFunctionType

P = 128
RUN = 8
PACK = 4
K_PASS = P * PACK
TOKENS, E, D, F = 4096, 1024, 512, 256
EPS = 1e-5
E_PASSES = E // K_PASS
GROUP_TILES = [2] * (TOKENS // P // 2 - 1) + [1, 1]
N_GROUPS = len(GROUP_TILES)
LOADED_FIRST = 6
WARM_UP = 3
VECTOR_SHARES_COPY = (3, 4)
ATTN_BANKS, Z_BANKS, X_BANKS, U_BANKS = 3, 2, 2, 1
FLOPS = 2 * TOKENS * (E * D + D * F)


def transpose_words(nc, bank, rows, ident):
    for b in range(rows.shape[1] // P):
        first = (b // 2) * 2 * P + b % 2
        nc.tensor.transpose(bank[:, b, :], rows[:, first : first + 2 * P - 1 : 2], ident)


def in_runs(rows):
    return rows.rearrange("p (q t i) -> p t q i", t=PACK, i=RUN)


def words_side_by_side(bank):
    return bank.rearrange("p (g u) c -> p g c u", u=2)


def tile_rotaryembeddingtransformerlayer_pb_t_kernel(
    tc, attn, src_norm, Wo, bo, g2, be2, W1, b1, out_0, out_1
):
    nc = tc.nc
    attn_tokens = attn.flatten_outer_dims()
    src_tokens = src_norm.flatten_outer_dims()
    x_tokens = out_0.flatten_outer_dims()
    u_tokens = out_1.flatten_outer_dims()

    def group_rows(tokens, n):
        first = P * sum(GROUP_TILES[:n])
        return tokens[first : first + P * GROUP_TILES[n], :].rearrange("(p j) c -> p j c", j=GROUP_TILES[n])

    with ExitStack() as ctx:
        ctx.enter_context(tc.manual_schedule())
        const = ctx.enter_context(tc.tile_pool(name="const", bufs=1))
        loads = ctx.enter_context(tc.tile_pool(name="loads", bufs=LOADED_FIRST + 1))
        work = ctx.enter_context(tc.tile_pool(name="work", bufs=2))
        x_pool = ctx.enter_context(tc.tile_pool(name="x_pool", bufs=6))
        u_pool = ctx.enter_context(tc.tile_pool(name="u_pool", bufs=3))
        stats = ctx.enter_context(tc.tile_pool(name="stats", bufs=4))
        psum = ctx.enter_context(tc.psum_pool(name="psum", bufs=1))

        ident = const.tile([P, P], F32)
        make_identity(nc, ident[:])
        ones = const.tile([P, D], BF16)
        nc.vector.memset(ones[:], 1.0)
        eps_col = const.tile([P, 1], F32)
        nc.vector.memset(eps_col[:], EPS)

        bias_row = const.tile([1, D + F], BF16)
        nc.sync.dma_start(out=bias_row[:, 0:D], in_=bo.rearrange("(o d) -> o d", o=1))
        nc.sync.dma_start(out=bias_row[:, D : D + F], in_=b1.rearrange("(o f) -> o f", o=1))
        wo_rows = const.tile([P, D // P, E], BF16)
        wo_chunks = Wo.rearrange("(c p) k -> c p k", p=P)
        for c in range(D // P):
            nc.sync.dma_start(out=wo_rows[:, c, :], in_=wo_chunks[c])
        bias_rows = const.tile([P, D + F], BF16)
        nc.vector.memset(bias_rows[:], 0.0)
        norm_rows = const.tile([P, P], BF16)
        nc.gpsimd.memset(norm_rows[:], 0.0)
        gain_shift = const.tile([P, 2 * PACK], F32)
        table_warm = const.tile([P, 1], F32)
        nc.scalar.activation(out=table_warm[:], in_=eps_col[:], func=ACT.Abs_reciprocal_sqrt)

        wo_words = wo_rows[:].bitcast(F32)
        wo_grouped = []
        for half in range(2):
            half_tile = const.tile([P, E_PASSES, D // 2, PACK], BF16, align_bytes=64, name=f"wo_grouped_{half}")
            wo_grouped.append(half_tile)
        wo_codes = const.tile([P, E_PASSES, D], U32, align_bytes=64)
        wo_scales = const.tile([P, E_PASSES, D], U8, align_bytes=64)

        def quantise_wo(half):
            rows = slice(half * (D // 2), (half + 1) * (D // 2))
            for g in range(E_PASSES):
                nc.vector.quantize_mx(
                    out=wo_codes[:, g, rows].bitcast(FP8X4),
                    scales=wo_scales[:, g, rows],
                    in_=wo_grouped[half][:, g].rearrange("p d t -> p (d t)"),
                )

        def transpose_wo_chunk(c):
            wo_bank = psum.tile([P, PACK, P], F32, tag="attn", bufs=ATTN_BANKS)
            transpose_words(nc, wo_bank, wo_words[:, c, :], ident[:])
            copy_out = nc.vector.tensor_copy if c == 1 else nc.scalar.copy
            half, place = divmod(c, 2)
            grouped_words = wo_grouped[half][:].bitcast(F32)
            copy_out(
                out=grouped_words[:, :, place * P : (place + 1) * P, :], in_=words_side_by_side(wo_bank[:])
            )

        bo_all = const.tile([P, D], F32)

        def keep_warm():
            idle_bank = psum.tile([P, D], F32, tag="u", bufs=U_BANKS)
            for _ in range(WARM_UP):
                nc.tensor.matmul(out=idle_bank[:], lhsT=ones[:, 0:P], rhs=ones[:], start=True, stop=True)

        def spread_bo():
            bo_bank = psum.tile([P, D], F32, tag="x", bufs=X_BANKS)
            nc.vector.tensor_copy(out=bias_rows[0:1, :], in_=bias_row[:])
            nc.tensor.matmul(out=bo_bank[:], lhsT=ones[:, 0:P], rhs=bias_rows[:, 0:D], start=True, stop=True)
            nc.vector.tensor_copy(out=bo_all[:], in_=bo_bank[:])

        b1_all = const.tile([P, F], F32)
        w1_rows = const.tile([P, F // P, D], BF16)
        w1_f32 = const.tile([P, F // P, PACK, P], F32)
        norm_rows_f32 = const.tile([P, P], F32)
        w1_grouped = const.tile([P, F, PACK], BF16, align_bytes=64)
        w1_codes = const.tile([P, F], U32, align_bytes=64)
        w1_scales = const.tile([P, F], U8, align_bytes=64)
        second_layer_banks = {}

        def load_second_layer():
            for first_row, vector in ((0, g2), (PACK, be2)):
                nc.sync.dma_start(
                    out=norm_rows[first_row : first_row + PACK, :].rearrange("t (q i) -> t q i", i=RUN),
                    in_=vector.rearrange("(q t i) -> t q i", t=PACK, i=RUN),
                )
            nc.sync.dma_start(out=w1_rows[:], in_=W1.rearrange("(c p) d -> p c d", p=P))

        def widen_w1():
            for c in range(F // P):
                nc.scalar.copy(out=w1_f32[:, c].rearrange("p t (q i) -> p t q i", i=RUN), in_=in_runs(w1_rows[:, c, :]))
            nc.scalar.copy(out=norm_rows_f32[:], in_=norm_rows[:])

        def transpose_w1():
            vectors_bank = psum.tile([P, F + P], F32, tag="u", bufs=U_BANKS)
            nc.tensor.transpose(vectors_bank[:, F : F + P], norm_rows_f32[:], ident[:])
            w1_banks = []
            for c in range(F // P):
                w1_bank = psum.tile([P, PACK, P], F32, tag="z", bufs=Z_BANKS)
                for t in range(PACK):
                    nc.tensor.transpose(w1_bank[:, t, :], w1_f32[:, c, t, :], ident[:])
                w1_banks.append(w1_bank)
            nc.tensor.matmul(
                out=vectors_bank[:, 0:F], lhsT=ones[:, 0:P], rhs=bias_rows[:, D : D + F], start=True, stop=True
            )
            second_layer_banks["vectors"], second_layer_banks["w1"] = vectors_bank, w1_banks

        def copy_w1():
            vectors_bank = second_layer_banks["vectors"]
            nc.scalar.copy(out=b1_all[:], in_=vectors_bank[:, 0:F])
            nc.scalar.copy(out=gain_shift[:], in_=vectors_bank[:, F : F + 2 * PACK])
            for c in range(F // P):
                nc.scalar.copy(
                    out=w1_grouped[:, c * P : (c + 1) * P, :],
                    in_=second_layer_banks["w1"][c][:].rearrange("p t f -> p f t"),
                )

        def quantise_w1():
            nc.vector.quantize_mx(
                out=w1_codes[:].bitcast(FP8X4),
                scales=w1_scales[:],
                in_=w1_grouped[:].rearrange("p f t -> p (f t)"),
            )

        attn_sb, src_sb, attn_banks, attn_grouped, attn_mx = {}, {}, {}, {}, {}
        x_sb, x_banks, row_sum, sum_sq, inv_std, shift_z = {}, {}, {}, {}, {}, {}
        z_sb, z_planes, h_planes, h_grouped, h_mx, u_banks, u_sb = {}, {}, {}, {}, {}, {}, {}

        def load(n):
            J = GROUP_TILES[n]
            attn_tile = loads.tile([P, J, E], BF16)
            nc.sync.dma_start(out=attn_tile[:], in_=group_rows(attn_tokens, n))
            src_tile = loads.tile([P, J, D], BF16)
            nc.sync.dma_start(out=src_tile[:], in_=group_rows(src_tokens, n))
            attn_sb[n], src_sb[n] = attn_tile, src_tile

        def transpose_attn(n):
            J = GROUP_TILES[n]
            attn_words = attn_sb[n][:].bitcast(F32)
            attn_banks[n] = []
            for j in range(J):
                attn_bank = psum.tile([P, PACK, P], F32, tag="attn", bufs=ATTN_BANKS)
                transpose_words(nc, attn_bank, attn_words[:, j, :], ident[:])
                attn_banks[n].append(attn_bank)

        def copy_attn(n):
            J = GROUP_TILES[n]
            attn_side = work.tile([P, J, E_PASSES, P, PACK], BF16, align_bytes=64)
            attn_side_words = attn_side[:].bitcast(F32)
            for j in range(J):
                copy_out = nc.vector.tensor_copy if n in VECTOR_SHARES_COPY and j == 1 else nc.scalar.copy
                copy_out(out=attn_side_words[:, j, :, :, :], in_=words_side_by_side(attn_banks[n][j][:]))
            attn_grouped[n] = attn_side

        def quantise_attn(n):
            J = GROUP_TILES[n]
            attn_codes = work.tile([P, J, E_PASSES, P], U32, align_bytes=64)
            attn_scales = work.tile([P, J, E_PASSES, P], U8, align_bytes=64)
            nc.vector.quantize_mx(
                out=attn_codes[:].rearrange("p j g k -> p (j g k)").bitcast(FP8X4),
                scales=attn_scales[:].rearrange("p j g k -> p (j g k)"),
                in_=attn_grouped[n][:].rearrange("p j g k t -> p (j g k t)"),
            )
            attn_mx[n] = (attn_codes, attn_scales)

        def residual(n):
            J = GROUP_TILES[n]
            x_tile = x_pool.tile([P, J, D], F32)
            nc.vector.tensor_tensor(
                out=x_tile[:], in0=src_sb[n][:], in1=bo_all[:].unsqueeze(1).to_broadcast([P, J, D]), op=ALU.add
            )
            x_sb[n] = x_tile

        def first_product(n):
            J = GROUP_TILES[n]
            codes, scales = attn_mx[n]
            x_banks[n] = []
            for j in range(J):
                x_bank = psum.tile([P, D], F32, tag="x", bufs=X_BANKS)
                for g in range(E_PASSES):
                    nc.tensor.matmul_mx(
                        out=x_bank[:],
                        lhsT=codes[:, j, g, :].bitcast(FP8X4),
                        lhsT_scale=scales[:, j, g, :],
                        rhs=wo_codes[:, g, :].bitcast(FP8X4),
                        rhs_scale=wo_scales[:, g, :],
                        start=(g == 0),
                        stop=(g == E_PASSES - 1),
                    )
                x_banks[n].append(x_bank)

        def finish_x(n):
            J = GROUP_TILES[n]
            sum_tile = stats.tile([P, J], F32)
            for j in range(J):
                nc.vector.scalar_tensor_tensor(
                    out=x_sb[n][:, j, :],
                    in0=x_banks[n][j][:],
                    scalar=0.0,
                    in1=x_sb[n][:, j, :],
                    op0=ALU.add,
                    op1=ALU.add,
                    accum_out=sum_tile[:, j : j + 1],
                )
            row_sum[n] = sum_tile

        def store_x(n):
            nc.sync.dma_start(out=group_rows(x_tokens, n), in_=x_sb[n][:])

        def squared_deviations(n):
            J = GROUP_TILES[n]
            squares = work.tile([P, J, D], BF16)
            sq_tile = stats.tile([P, J], F32)
            for j in range(J):
                nc.scalar.activation(
                    out=squares[:, j, :],
                    in_=x_sb[n][:, j, :],
                    func=ACT.Square,
                    scale=-float(D),
                    bias=row_sum[n][:, j : j + 1],
                    accum_out=sq_tile[:, j : j + 1],
                )
            sum_sq[n] = sq_tile

        def invert_std(n):
            J = GROUP_TILES[n]
            inv_tile = stats.tile([P, J], F32)
            nc.scalar.activation(
                out=inv_tile[:], in_=sum_sq[n][:], func=ACT.Abs_reciprocal_sqrt, scale=1.0 / D**3, bias=eps_col[:]
            )
            inv_std[n] = inv_tile

        def shift_of_z(n):
            J = GROUP_TILES[n]
            shift_tile = stats.tile([P, J], F32)
            shift_z[n] = shift_tile
            if n == N_GROUPS - 1:
                nc.vector.scalar_tensor_tensor(
                    out=shift_tile[:],
                    in0=row_sum[n][:],
                    scalar=-1.0 / D,
                    in1=inv_std[n][:],
                    op0=ALU.mult,
                    op1=ALU.mult,
                )
                return
            mean_tile = stats.tile([P, J], F32)
            nc.gpsimd.tensor_scalar(
                out=mean_tile[:], in0=row_sum[n][:], scalar1=-1.0 / D, scalar2=0.0, op0=ALU.mult, op1=ALU.add
            )
            nc.gpsimd.tensor_tensor(out=shift_tile[:], in0=mean_tile[:], in1=inv_std[n][:], op=ALU.mult)

        def z_in_runs(z_tile, j):
            return z_tile[:, j].rearrange("p t (q i) -> p t q i", i=RUN)

        def normalise_early(n):
            J = GROUP_TILES[n]
            z_tile = work.tile([P, J, PACK, P], F32)
            z_sb[n] = z_tile
            draining = n >= N_GROUPS - 2
            engine = nc.vector if draining else nc.gpsimd
            for j in range(J if draining else 1):
                engine.tensor_scalar(
                    out=z_in_runs(z_tile, j),
                    in0=in_runs(x_sb[n][:, j, :]),
                    scalar1=inv_std[n][:, j : j + 1],
                    scalar2=shift_z[n][:, j : j + 1],
                    op0=ALU.mult,
                    op1=ALU.add,
                )

        def normalise_late(n):
            if n < N_GROUPS - 2:
                nc.scalar.activation(
                    out=z_in_runs(z_sb[n], 1),
                    in_=in_runs(x_sb[n][:, 1, :]),
                    func=ACT.Identity,
                    scale=inv_std[n][:, 1:2],
                    bias=shift_z[n][:, 1:2],
                )

        def transpose_z(n):
            J = GROUP_TILES[n]
            banks = []
            for b in range(J):
                z_bank = psum.tile([P, PACK // J, J * P], F32, tag="z", bufs=Z_BANKS)
                banks.append(z_bank)
            z_planes[n] = [banks[t * J // PACK][:, t % (PACK // J), :] for t in range(PACK)]
            for j in range(J):
                for t in range(PACK):
                    nc.tensor.transpose(
                        z_planes[n][t][:, j * P : (j + 1) * P],
                        z_sb[n][:, j, t, :],
                        ident[:],
                    )

        def gain_and_shift(n):
            J = GROUP_TILES[n]
            planes = work.tile([P, PACK, J * P], BF16)
            for t in range(PACK):
                nc.scalar.activation(
                    out=planes[:, t, :],
                    in_=z_planes[n][t],
                    func=ACT.Identity,
                    scale=gain_shift[:, t : t + 1],
                    bias=gain_shift[:, PACK + t : PACK + t + 1],
                )
            h_planes[n] = planes

        def regroup_h(n):
            J = GROUP_TILES[n]
            h_side = work.tile([P, J * P, PACK], BF16, align_bytes=64)
            nc.vector.tensor_copy(
                out=h_side[:].rearrange("p (c i) t -> p c t i", i=4),
                in_=h_planes[n][:].rearrange("p t (c i) -> p c t i", i=4),
            )
            h_grouped[n] = h_side

        def quantise_h(n):
            J = GROUP_TILES[n]
            h_codes = work.tile([P, J * P], U32, align_bytes=64)
            h_scales = work.tile([P, J * P], U8, align_bytes=64)
            nc.vector.quantize_mx(
                out=h_codes[:].bitcast(FP8X4), scales=h_scales[:], in_=h_grouped[n][:].rearrange("p k t -> p (k t)")
            )
            h_mx[n] = (h_codes, h_scales)

        def second_product(n):
            J = GROUP_TILES[n]
            codes, scales = h_mx[n]
            u_bank = psum.tile([P, J, F], F32, tag="u", bufs=U_BANKS)
            for j in range(J):
                nc.tensor.matmul_mx(
                    out=u_bank[:, j, :],
                    lhsT=codes[:, j * P : (j + 1) * P].bitcast(FP8X4),
                    lhsT_scale=scales[:, j * P : (j + 1) * P],
                    rhs=w1_codes[:].bitcast(FP8X4),
                    rhs_scale=w1_scales[:],
                    start=True,
                    stop=True,
                )
            u_banks[n] = u_bank

        def add_b1(n):
            J = GROUP_TILES[n]
            u_tile = u_pool.tile([P, J, F], F32)
            nc.vector.tensor_tensor(
                out=u_tile[:], in0=u_banks[n][:], in1=b1_all[:].unsqueeze(1).to_broadcast([P, J, F]), op=ALU.add
            )
            u_sb[n] = u_tile

        def relu_and_store_u(n):
            if n % 2 == 0 and n < N_GROUPS - 1:
                nc.scalar.activation(out=u_sb[n][:], in_=u_sb[n][:], func=ACT.Relu)
            else:
                nc.vector.tensor_scalar_max(out=u_sb[n][:], in0=u_sb[n][:], scalar1=0.0)
            nc.sync.dma_start(out=group_rows(u_tokens, n), in_=u_sb[n][:])

        def exists(n):
            return 0 <= n < N_GROUPS

        def run(stage, n):
            if exists(n):
                stage(n)

        for n in range(LOADED_FIRST):
            load(n)
            if n == 1:
                load_second_layer()
        keep_warm()
        spread_bo()
        for c in range(D // P):
            transpose_wo_chunk(c)
            if c == 1:
                quantise_wo(0)
        transpose_attn(0)
        quantise_wo(1)
        copy_attn(0)
        transpose_attn(1)
        residual(0)
        quantise_attn(0)
        keep_warm()
        first_product(0)
        copy_attn(1)
        widen_w1()
        residual(1)
        quantise_attn(1)
        transpose_attn(2)
        copy_attn(2)

        for r in range(N_GROUPS + 3):
            run(load, r + LOADED_FIRST)
            run(gain_and_shift, r - 2)
            run(finish_x, r)
            run(store_x, r)
            run(first_product, r + 1)
            run(normalise_early, r - 1)
            if r == 0:
                transpose_attn(3)
                transpose_w1()
            run(add_b1, r - 3)
            run(quantise_attn, r + 2)
            run(regroup_h, r - 2)
            run(residual, r + 2)
            run(quantise_h, r - 2)
            run(copy_attn, r + 3)
            run(normalise_late, r - 1)
            run(transpose_attn, r + 4)
            run(transpose_z, r - 1)
            run(second_product, r - 2)
            run(squared_deviations, r)
            run(invert_std, r)
            run(shift_of_z, r)
            run(relu_and_store_u, r - 3)
            if r == 0:
                copy_w1()
            if r == 1:
                quantise_w1()
